import numpy as np
import ml_dtypes


def mxq(x, axis, fmt="e4m3"):
    dtype, down = {"e4m3": (ml_dtypes.float8_e4m3fn, 7), "e5m2": (ml_dtypes.float8_e5m2, 14)}[fmt]
    v = np.moveaxis(np.asarray(x, np.float32).astype(ml_dtypes.bfloat16).astype(np.float64), axis, -1)
    blocks = v.reshape(v.shape[:-1] + (-1, 32))
    amax = np.abs(blocks).max(-1, keepdims=True)
    byte = np.maximum(np.where(amax > 0, np.frexp(amax)[1] - 1 + 127, 0) - down, 1)
    scale = np.exp2(byte - 127.0)
    codes = (blocks / scale).astype(np.float32).astype(dtype).astype(np.float64)
    return np.moveaxis((codes * scale).reshape(v.shape), -1, axis)


WIDE = False


def mx_kscale(k):
    if not WIDE:
        return np.ones(k)
    levels = np.array([10, -10, 5, -5, 0])
    if k % 512:
        return np.exp2(np.random.permutation(np.resize(levels, k // 32))).repeat(32)
    a = np.empty((k // 512, 16))
    for p in range(k // 512):
        a[p, :8] = np.random.permutation(np.resize(levels, 8))
        for g in range(8):
            far = levels[np.abs(levels - a[p, g]) >= 10]
            a[p, g + 8] = far[np.random.randint(len(far))]
    return np.exp2(a.ravel()).repeat(32)


BF16 = ml_dtypes.bfloat16


def bf(x):
    return np.asarray(x, np.float32).astype(BF16)


def f64(x):
    return np.asarray(x).astype(np.float64)


B, NQ = 256, 12
CONTROL = 0
DIM = 1 << NQ
HALF = DIM // 2


def setup_inputs():
    on = np.nonzero((np.arange(DIM) & (1 << (NQ - CONTROL - 1))) != 0)[0]
    sv = np.ones(DIM)
    sv[on] = mx_kscale(HALF)
    return {"state": bf(np.random.standard_normal((B, DIM)) * sv),
            "target_matrix": bf(np.random.standard_normal((DIM, DIM)) / np.sqrt(HALF) / sv[:, None]),
            "control": CONTROL,
            "num_qubits": NQ}


def core(state, target_matrix, control, num_qubits):
    dim = 1 << num_qubits
    mask = 1 << (num_qubits - control - 1)
    c1_mask = (np.arange(dim) & mask) != 0
    on = np.nonzero(c1_mask)[0]
    st, tm = f64(state), f64(target_matrix)
    transformed = mxq(st[:, on], 1, "e4m3") @ mxq(tm[np.ix_(on, on)], 0, "e4m3")
    out = st.copy()
    out[:, on] = transformed
    return out


def e4m3fn_bytes(y):
    return np.clip(np.asarray(y, np.float64), -448.0, 448.0).astype(np.float32).astype(ml_dtypes.float8_e4m3fn).view(np.uint8)


def reference(state, target_matrix, control, num_qubits):
    out = core(state, target_matrix, control, num_qubits)
    s = np.max(np.abs(out)) / 448.0
    return out, e4m3fn_bytes(out / s)

@@ -1,0 +1,231 @@
+from contextlib import ExitStack
+
+import concourse.mybir as mybir
+from concourse.masks import make_identity
+
+F32 = mybir.dt.float32
+BF16 = mybir.dt.bfloat16
+U32 = mybir.dt.uint32
+U8 = mybir.dt.uint8
+FP8X4 = mybir.dt.float8_e4m3fn_x4
+FP8 = mybir.dt.float8_e4m3fn
+ALU = mybir.AluOpType
+ACT = mybir.ActivationFunctionType
+AX = mybir.AxisListType
+
+P = 128
+B = 256
+DIM = 4096
+HALF = 2048
+PASSES = 4
+K_PASS = 512
+NT = 512
+NCH = HALF // NT
+MT = B // P
+
+FLOPS = 2 * B * HALF * HALF
+BYTES = B * DIM * 2 + HALF * HALF * 2 + B * DIM * 4 + B * DIM
+
+V_COLS = 240
+GROUPED_BUFS = 4
+LOAD_WIDTHS = ((512, 512, 1024), (1024, 1024), (1024, 1024), (1024, 1024))
+EVAC_LAG = 2
+AMAX_LAG = 3
+CAST_PIECES = ((0, 0, 2048), (0, 2048, 2048), (1, 0, 2048), (1, 2048, 1024), (1, 3072, 1024))
+CAST_V_SHARE = 0.67
+
+
+def tile_builtcontrolled_kernel(tc, state, target_matrix, control, num_qubits, out_0, out_1):
+    nc = tc.nc
+    with ExitStack() as ctx:
+        keep = ctx.enter_context(tc.tile_pool(name="keep", bufs=1))
+        stage = ctx.enter_context(tc.tile_pool(name="stage", bufs=GROUPED_BUFS))
+        psum = ctx.enter_context(tc.psum_pool(name="psum", bufs=1))
+        ctx.enter_context(tc.manual_schedule())
+
+        ident = keep.tile([P, P], F32, name="ident")
+        make_identity(nc, ident[:])
+        zero = keep.tile([P, 1], F32, name="zero")
+        nc.vector.memset(zero[:], 0.0)
+        warm = keep.tile([P, 1], F32, name="warm")
+        nc.scalar.activation(out=warm[:], in_=zero[:], func=ACT.Identity, scale=zero[:, 0:1], bias=zero[:, 0:1])
+
+        xl = {}
+        xr = {}
+        for m in range(MT):
+            rows = slice(m * P, (m + 1) * P)
+            for h in range(2):
+                xl[(m, h)] = keep.tile([P, 1024], BF16, name="xl%d%d" % (m, h))
+                nc.sync.dma_start(out=xl[(m, h)][:], in_=state[rows, 1024 * h:1024 * (h + 1)])
+            for h in range(2):
+                xr[(m, h)] = keep.tile([P, 1024], BF16, name="xr%d%d" % (m, h))
+                nc.sync.dma_start(out=xr[(m, h)][:], in_=state[rows, HALF + 1024 * h:HALF + 1024 * (h + 1)])
+        raw_of = {}
+        for g in range(PASSES):
+            c0 = 0
+            for d, width in enumerate(LOAD_WIDTHS[g]):
+                raw = keep.tile([P, 4, width], BF16, name="raw%d%d" % (g, d))
+                nc.sync.dma_start(
+                    out=raw[:],
+                    in_=target_matrix[HALF + K_PASS * g:HALF + K_PASS * (g + 1), HALF + c0:HALF + c0 + width]
+                    .rearrange("(p j) w -> p j w", j=4),
+                )
+                for c in range(c0 // NT, (c0 + width) // NT):
+                    raw_of[(g, c)] = (raw, c * NT - c0)
+                c0 += width
+
+        t_codes = keep.tile([P, PASSES * HALF], U32, name="t_codes", align_bytes=64)
+        t_scales = keep.tile([P, PASSES * HALF], U8, name="t_scales", align_bytes=64)
+        x_codes = keep.tile([P, MT * PASSES * P], U32, name="x_codes", align_bytes=64)
+        x_scales = keep.tile([P, MT * PASSES * P], U8, name="x_scales", align_bytes=64)
+        o = [keep.tile([P, DIM], F32, name="o%d" % m) for m in range(MT)]
+        q8 = [keep.tile([P, DIM], FP8, name="q8%d" % m) for m in range(MT)]
+        n_stats = 4 + MT * NCH
+        stats = keep.tile([P, n_stats], F32, name="stats")
+
+        def left_amax(m, h):
+            i = 2 * m + h
+            nc.vector.tensor_reduce(out=stats[:, i:i + 1], in_=xl[(m, h)][:], axis=AX.X, op=ALU.max,
+                                    apply_absolute_value=True)
+
+        def left_widen(m, h):
+            dst = o[m][:, 1024 * h:1024 * (h + 1)]
+            if m == 0:
+                nc.scalar.copy(out=dst, in_=xl[(m, h)][:])
+            else:
+                nc.gpsimd.tensor_scalar(out=dst, in0=xl[(m, h)][:], scalar1=1.0, scalar2=0.0,
+                                        op0=ALU.mult, op1=ALU.add)
+
+        def left_store(m, h):
+            nc.sync.dma_start(out=out_0[m * P:(m + 1) * P, 1024 * h:1024 * (h + 1)],
+                              in_=o[m][:, 1024 * h:1024 * (h + 1)])
+
+        xt = {}
+        xg = {}
+        XT_BANK = {(0, 0): 2, (0, 1): 3, (1, 0): 6, (1, 1): 7}
+
+        def x_transpose(m, h):
+            words = xr[(m, h)][:].bitcast(F32)
+            xt[(m, h)] = psum.tile([P, 2, 2, P], F32, name="xt%d%d" % (m, h), tag="bank%d" % XT_BANK[(m, h)])
+            for gi in range(2):
+                for u in range(2):
+                    nc.tensor.transpose(xt[(m, h)][:, gi, u, :], words[:, 256 * gi + u:256 * (gi + 1):2], ident[:])
+
+        def x_evac(m, h):
+            xg[(m, h)] = keep.tile([P, 2, P, 4], BF16, name="xg%d%d" % (m, h), align_bytes=64)
+            nc.scalar.copy(out=xg[(m, h)][:].bitcast(F32), in_=xt[(m, h)][:].rearrange("p g u r -> p g r u"))
+
+        def x_quant(m, h):
+            base = (m * PASSES + 2 * h) * P
+            nc.vector.quantize_mx(
+                out=x_codes[:, base:base + 2 * P].bitcast(FP8X4),
+                scales=x_scales[:, base:base + 2 * P],
+                in_=xg[(m, h)][:].rearrange("p g r j -> p (g r j)"),
+            )
+
+        units = [(g, c) for g in range(PASSES) for c in range(NCH)]
+        grouped = {}
+        acc = {}
+
+        def interleave(k):
+            g, c = units[k]
+            raw, c0 = raw_of[(g, c)]
+            grp = stage.tile([P, NT, 4], BF16, name="grp", align_bytes=64)
+            grouped[k] = grp
+            nc.vector.tensor_copy(out=grp[:, 0:V_COLS, :],
+                                  in_=raw[:, :, c0:c0 + V_COLS].rearrange("p j w -> p w j"))
+            nc.scalar.copy(out=grp[:, V_COLS:NT, :],
+                           in_=raw[:, :, c0 + V_COLS:c0 + NT].rearrange("p j w -> p w j"))
+
+        def quantize(k):
+            g, c = units[k]
+            tb = g * HALF + c * NT
+            nc.vector.quantize_mx(
+                out=t_codes[:, tb:tb + NT].bitcast(FP8X4),
+                scales=t_scales[:, tb:tb + NT],
+                in_=grouped[k][:].rearrange("p w j -> p (w j)"),
+            )
+
+        def multiply(k):
+            g, c = units[k]
+            tb = g * HALF + c * NT
+            for m in range(MT):
+                if g == 0:
+                    acc[(m, c)] = psum.tile([P, NT], F32, name="acc%d%d" % (m, c), tag="bank%d" % (NCH * m + c))
+                xb = (m * PASSES + g) * P
+                nc.tensor.matmul_mx(
+                    out=acc[(m, c)][:],
+                    lhsT=x_codes[:, xb:xb + P].bitcast(FP8X4),
+                    lhsT_scale=x_scales[:, xb:xb + P],
+                    rhs=t_codes[:, tb:tb + NT].bitcast(FP8X4),
+                    rhs_scale=t_scales[:, tb:tb + NT],
+                    start=(g == 0),
+                    stop=(g == PASSES - 1),
+                )
+
+        def right_evac(c):
+            for m in range(MT):
+                nc.scalar.copy(out=o[m][:, HALF + c * NT:HALF + (c + 1) * NT], in_=acc[(m, c)][:])
+
+        def right_amax_store(c):
+            for m in range(MT):
+                i = 4 + NCH * m + c
+                cols = slice(HALF + c * NT, HALF + (c + 1) * NT)
+                nc.vector.tensor_reduce(out=stats[:, i:i + 1], in_=o[m][:, cols], axis=AX.X, op=ALU.max,
+                                        apply_absolute_value=True)
+                nc.sync.dma_start(out=out_0[m * P:(m + 1) * P, cols], in_=o[m][:, cols])
+
+        for h in range(2):
+            left_amax(0, h)
+            left_widen(0, h)
+            left_store(0, h)
+        x_transpose(0, 0)
+        x_transpose(0, 1)
+        x_evac(0, 0)
+        x_evac(0, 1)
+        for h in range(2):
+            left_amax(1, h)
+            left_widen(1, h)
+            left_store(1, h)
+        x_transpose(1, 0)
+        x_transpose(1, 1)
+        x_evac(1, 0)
+        x_quant(0, 0)
+        x_quant(0, 1)
+
+        n_units = len(units)
+        first_last = n_units - NCH
+        for k in range(n_units + AMAX_LAG):
+            if k < n_units:
+                interleave(k)
+            if k == 0:
+                x_quant(1, 0)
+                x_evac(1, 1)
+            if k == 1:
+                x_quant(1, 1)
+            if 0 <= k - 1 < n_units:
+                quantize(k - 1)
+                multiply(k - 1)
+            if first_last <= k - EVAC_LAG < n_units:
+                right_evac(k - EVAC_LAG - first_last)
+            if first_last <= k - AMAX_LAG < n_units:
+                right_amax_store(k - AMAX_LAG - first_last)
+
+        part = keep.tile([P, 1], F32, name="part")
+        nc.vector.tensor_reduce(out=part[:], in_=stats[:], axis=AX.X, op=ALU.max)
+        spread = psum.tile([P, P], F32, name="spread", tag="bank0")
+        nc.tensor.transpose(spread[:], part[:, 0:1].to_broadcast([P, P]), ident[:])
+        amax = keep.tile([P, 1], F32, name="amax")
+        nc.vector.tensor_reduce(out=amax[:], in_=spread[:], axis=AX.X, op=ALU.max)
+        rinv = keep.tile([P, 1], F32, name="rinv")
+        nc.vector.reciprocal(out=rinv[:], in_=amax[:])
+        factor = keep.tile([P, 1], F32, name="factor")
+        nc.vector.tensor_scalar(out=factor[:], in0=rinv[:], scalar1=448.0, scalar2=None, op0=ALU.mult)
+
+        for m, a, width in CAST_PIECES:
+            vw = int(width * CAST_V_SHARE) // 16 * 16
+            nc.vector.tensor_scalar(out=q8[m][:, a:a + vw], in0=o[m][:, a:a + vw], scalar1=factor[:, 0:1],
+                                    scalar2=None, op0=ALU.mult, saturate=False)
+            nc.scalar.activation(out=q8[m][:, a + vw:a + width], in_=o[m][:, a + vw:a + width], func=ACT.Identity,
+                                 scale=factor[:, 0:1], bias=zero[:, 0:1], saturate=False)
+            nc.sync.dma_start(out=out_1[m * P:(m + 1) * P, a:a + width], in_=q8[m][:, a:a + width].bitcast(U8))

@@ -132,10 +132,10 @@ def tile_builtcontrolled_kernel(tc, state, target_matrix, control, num_qubits, o
             raw, c0 = raw_of[(g, c)]
             grp = stage.tile([P, NT, 4], BF16, name="grp", align_bytes=64)
             grouped[k] = grp
-            nc.vector.tensor_copy(out=grp[:, 0:V_COLS, :],
-                                  in_=raw[:, :, c0:c0 + V_COLS].rearrange("p j w -> p w j"))
-            nc.scalar.copy(out=grp[:, V_COLS:NT, :],
-                           in_=raw[:, :, c0 + V_COLS:c0 + NT].rearrange("p j w -> p w j"))
+            nc.vector.tensor_copy(out=grp[:, 0:V_COLS, :].rearrange("p (c i) t -> p c t i", i=4),
+                                  in_=raw[:, :, c0:c0 + V_COLS].rearrange("p t (c i) -> p c t i", i=4))
+            nc.scalar.copy(out=grp[:, V_COLS:NT, :].rearrange("p (c i) t -> p c t i", i=4),
+                           in_=raw[:, :, c0 + V_COLS:c0 + NT].rearrange("p t (c i) -> p c t i", i=4))
 
         def quantize(k):
             g, c = units[k]

@@ -26,9 +26,13 @@ MT = B // P
 FLOPS = 2 * B * HALF * HALF
 BYTES = B * DIM * 2 + HALF * HALF * 2 + B * DIM * 4 + B * DIM
 
-V_COLS = 240
-GROUPED_BUFS = 4
-LOAD_WIDTHS = ((512, 512, 1024), (1024, 1024), (1024, 1024), (1024, 1024))
+UNITS = (
+    (0, 0, 512, 352), (0, 512, 512, 240), (0, 1024, 1024, 528),
+    (1, 0, 1024, 512), (1, 1024, 1024, 512),
+    (2, 0, 1024, 496), (2, 1024, 1024, 480),
+    (3, 0, 1024, 480), (3, 1024, 512, 240), (3, 1536, 512, 288),
+)
+GROUPED_BUFS = 3
 EVAC_LAG = 2
 AMAX_LAG = 3
 CAST_PIECES = ((0, 0, 2048), (0, 2048, 2048), (1, 0, 2048), (1, 2048, 1024), (1, 3072, 1024))
@@ -50,177 +54,164 @@ def tile_builtcontrolled_kernel(tc, state, target_matrix, control, num_qubits, o
         warm = keep.tile([P, 1], F32, name="warm")
         nc.scalar.activation(out=warm[:], in_=zero[:], func=ACT.Identity, scale=zero[:, 0:1], bias=zero[:, 0:1])
 
-        xl = {}
-        xr = {}
-        for m in range(MT):
-            rows = slice(m * P, (m + 1) * P)
-            for h in range(2):
-                xl[(m, h)] = keep.tile([P, 1024], BF16, name="xl%d%d" % (m, h))
-                nc.sync.dma_start(out=xl[(m, h)][:], in_=state[rows, 1024 * h:1024 * (h + 1)])
-            for h in range(2):
-                xr[(m, h)] = keep.tile([P, 1024], BF16, name="xr%d%d" % (m, h))
-                nc.sync.dma_start(out=xr[(m, h)][:], in_=state[rows, HALF + 1024 * h:HALF + 1024 * (h + 1)])
-        raw_of = {}
-        for g in range(PASSES):
-            c0 = 0
-            for d, width in enumerate(LOAD_WIDTHS[g]):
-                raw = keep.tile([P, 4, width], BF16, name="raw%d%d" % (g, d))
-                nc.sync.dma_start(
-                    out=raw[:],
-                    in_=target_matrix[HALF + K_PASS * g:HALF + K_PASS * (g + 1), HALF + c0:HALF + c0 + width]
-                    .rearrange("(p j) w -> p j w", j=4),
-                )
-                for c in range(c0 // NT, (c0 + width) // NT):
-                    raw_of[(g, c)] = (raw, c * NT - c0)
-                c0 += width
+        xl0 = [keep.tile([P, 1024], BF16, name="xl0%d" % h) for h in range(2)]
+        xl1 = keep.tile([P, HALF], BF16, name="xl1")
+        xr = [keep.tile([P, HALF], BF16, name="xr%d" % m) for m in range(MT)]
+        for h in range(2):
+            nc.sync.dma_start(out=xl0[h][:], in_=state[0:P, 1024 * h:1024 * (h + 1)])
+        nc.sync.dma_start(out=xr[0][:], in_=state[0:P, HALF:DIM])
+        nc.sync.dma_start(out=xl1[:], in_=state[P:B, 0:HALF])
+        nc.sync.dma_start(out=xr[1][:], in_=state[P:B, HALF:DIM])
+        raws = []
+        for k, (g, c0, width, v_cols) in enumerate(UNITS):
+            raw = keep.tile([P, 4, width], BF16, name="raw%d" % k)
+            nc.sync.dma_start(
+                out=raw[:],
+                in_=target_matrix[HALF + K_PASS * g:HALF + K_PASS * (g + 1), HALF + c0:HALF + c0 + width]
+                .rearrange("(p j) w -> p j w", j=4),
+            )
+            raws.append(raw)
 
         t_codes = keep.tile([P, PASSES * HALF], U32, name="t_codes", align_bytes=64)
         t_scales = keep.tile([P, PASSES * HALF], U8, name="t_scales", align_bytes=64)
         x_codes = keep.tile([P, MT * PASSES * P], U32, name="x_codes", align_bytes=64)
         x_scales = keep.tile([P, MT * PASSES * P], U8, name="x_scales", align_bytes=64)
+        xg = [keep.tile([P, PASSES, P, 4], BF16, name="xg%d" % m, align_bytes=64) for m in range(MT)]
         o = [keep.tile([P, DIM], F32, name="o%d" % m) for m in range(MT)]
         q8 = [keep.tile([P, DIM], FP8, name="q8%d" % m) for m in range(MT)]
-        n_stats = 4 + MT * NCH
-        stats = keep.tile([P, n_stats], F32, name="stats")
+        N_STATS = 9
+        stats = keep.tile([P, N_STATS], F32, name="stats")
+        n_used = [0]
 
-        def left_amax(m, h):
-            i = 2 * m + h
-            nc.vector.tensor_reduce(out=stats[:, i:i + 1], in_=xl[(m, h)][:], axis=AX.X, op=ALU.max,
-                                    apply_absolute_value=True)
-
-        def left_widen(m, h):
-            dst = o[m][:, 1024 * h:1024 * (h + 1)]
-            if m == 0:
-                nc.scalar.copy(out=dst, in_=xl[(m, h)][:])
-            else:
-                nc.gpsimd.tensor_scalar(out=dst, in0=xl[(m, h)][:], scalar1=1.0, scalar2=0.0,
-                                        op0=ALU.mult, op1=ALU.add)
-
-        def left_store(m, h):
-            nc.sync.dma_start(out=out_0[m * P:(m + 1) * P, 1024 * h:1024 * (h + 1)],
-                              in_=o[m][:, 1024 * h:1024 * (h + 1)])
+        def abs_max(src):
+            i = n_used[0]
+            n_used[0] = i + 1
+            nc.vector.tensor_reduce(out=stats[:, i:i + 1], in_=src, axis=AX.X, op=ALU.max, apply_absolute_value=True)
 
         xt = {}
-        xg = {}
         XT_BANK = {(0, 0): 2, (0, 1): 3, (1, 0): 6, (1, 1): 7}
 
         def x_transpose(m, h):
-            words = xr[(m, h)][:].bitcast(F32)
+            words = xr[m][:].bitcast(F32)
             xt[(m, h)] = psum.tile([P, 2, 2, P], F32, name="xt%d%d" % (m, h), tag="bank%d" % XT_BANK[(m, h)])
             for gi in range(2):
+                g = 2 * h + gi
                 for u in range(2):
-                    nc.tensor.transpose(xt[(m, h)][:, gi, u, :], words[:, 256 * gi + u:256 * (gi + 1):2], ident[:])
+                    nc.tensor.transpose(xt[(m, h)][:, gi, u, :], words[:, 256 * g + u:256 * (g + 1):2], ident[:])
 
         def x_evac(m, h):
-            xg[(m, h)] = keep.tile([P, 2, P, 4], BF16, name="xg%d%d" % (m, h), align_bytes=64)
-            nc.scalar.copy(out=xg[(m, h)][:].bitcast(F32), in_=xt[(m, h)][:].rearrange("p g u r -> p g r u"))
+            nc.scalar.copy(out=xg[m][:, 2 * h:2 * h + 2, :, :].bitcast(F32),
+                           in_=xt[(m, h)][:].rearrange("p g u r -> p g r u"))
 
-        def x_quant(m, h):
-            base = (m * PASSES + 2 * h) * P
+        def x_quant(m):
+            base = m * PASSES * P
             nc.vector.quantize_mx(
-                out=x_codes[:, base:base + 2 * P].bitcast(FP8X4),
-                scales=x_scales[:, base:base + 2 * P],
-                in_=xg[(m, h)][:].rearrange("p g r j -> p (g r j)"),
+                out=x_codes[:, base:base + PASSES * P].bitcast(FP8X4),
+                scales=x_scales[:, base:base + PASSES * P],
+                in_=xg[m][:].rearrange("p g r j -> p (g r j)"),
             )
 
-        units = [(g, c) for g in range(PASSES) for c in range(NCH)]
         grouped = {}
         acc = {}
 
         def interleave(k):
-            g, c = units[k]
-            raw, c0 = raw_of[(g, c)]
-            grp = stage.tile([P, NT, 4], BF16, name="grp", align_bytes=64)
+            g, c0, width, v_cols = UNITS[k]
+            raw = raws[k]
+            grp = stage.tile([P, width, 4], BF16, name="grp", align_bytes=64)
             grouped[k] = grp
-            nc.vector.tensor_copy(out=grp[:, 0:V_COLS, :].rearrange("p (c i) t -> p c t i", i=4),
-                                  in_=raw[:, :, c0:c0 + V_COLS].rearrange("p t (c i) -> p c t i", i=4))
-            nc.scalar.copy(out=grp[:, V_COLS:NT, :].rearrange("p (c i) t -> p c t i", i=4),
-                           in_=raw[:, :, c0 + V_COLS:c0 + NT].rearrange("p t (c i) -> p c t i", i=4))
+            nc.vector.tensor_copy(out=grp[:, 0:v_cols, :].rearrange("p (c i) t -> p c t i", i=4),
+                                  in_=raw[:, :, 0:v_cols].rearrange("p t (c i) -> p c t i", i=4))
+            nc.scalar.copy(out=grp[:, v_cols:width, :].rearrange("p (c i) t -> p c t i", i=4),
+                           in_=raw[:, :, v_cols:width].rearrange("p t (c i) -> p c t i", i=4))
 
         def quantize(k):
-            g, c = units[k]
-            tb = g * HALF + c * NT
+            g, c0, width, v_cols = UNITS[k]
+            tb = g * HALF + c0
             nc.vector.quantize_mx(
-                out=t_codes[:, tb:tb + NT].bitcast(FP8X4),
-                scales=t_scales[:, tb:tb + NT],
+                out=t_codes[:, tb:tb + width].bitcast(FP8X4),
+                scales=t_scales[:, tb:tb + width],
                 in_=grouped[k][:].rearrange("p w j -> p (w j)"),
             )
 
         def multiply(k):
-            g, c = units[k]
-            tb = g * HALF + c * NT
-            for m in range(MT):
-                if g == 0:
-                    acc[(m, c)] = psum.tile([P, NT], F32, name="acc%d%d" % (m, c), tag="bank%d" % (NCH * m + c))
-                xb = (m * PASSES + g) * P
-                nc.tensor.matmul_mx(
-                    out=acc[(m, c)][:],
-                    lhsT=x_codes[:, xb:xb + P].bitcast(FP8X4),
-                    lhsT_scale=x_scales[:, xb:xb + P],
-                    rhs=t_codes[:, tb:tb + NT].bitcast(FP8X4),
-                    rhs_scale=t_scales[:, tb:tb + NT],
-                    start=(g == 0),
-                    stop=(g == PASSES - 1),
-                )
+            g, c0, width, v_cols = UNITS[k]
+            for c in range(c0 // NT, (c0 + width) // NT):
+                tb = g * HALF + c * NT
+                for m in range(MT):
+                    if g == 0:
+                        acc[(m, c)] = psum.tile([P, NT], F32, name="acc%d%d" % (m, c), tag="bank%d" % (NCH * m + c))
+                    xb = (m * PASSES + g) * P
+                    nc.tensor.matmul_mx(
+                        out=acc[(m, c)][:],
+                        lhsT=x_codes[:, xb:xb + P].bitcast(FP8X4),
+                        lhsT_scale=x_scales[:, xb:xb + P],
+                        rhs=t_codes[:, tb:tb + NT].bitcast(FP8X4),
+                        rhs_scale=t_scales[:, tb:tb + NT],
+                        start=(g == 0),
+                        stop=(g == PASSES - 1),
+                    )
 
-        def right_evac(c):
+        def right_evac(k):
+            g, c0, width, v_cols = UNITS[k]
             for m in range(MT):
-                nc.scalar.copy(out=o[m][:, HALF + c * NT:HALF + (c + 1) * NT], in_=acc[(m, c)][:])
+                for c in range(c0 // NT, (c0 + width) // NT):
+                    nc.scalar.copy(out=o[m][:, HALF + c * NT:HALF + (c + 1) * NT], in_=acc[(m, c)][:])
+                    if (m, c) != (0, 0):
+                        busy = psum.tile([P, NT], F32, name="busy%d%d" % (m, c), tag="bank%d" % (NCH * m + c))
+                        nc.tensor.matmul(out=busy[:], lhsT=xl0[0][:, 0:P], rhs=xl0[0][:, 0:NT], start=True, stop=True)
 
-        def right_amax_store(c):
+        def right_amax_store(k):
+            g, c0, width, v_cols = UNITS[k]
+            cols = slice(HALF + c0, HALF + c0 + width)
             for m in range(MT):
-                i = 4 + NCH * m + c
-                cols = slice(HALF + c * NT, HALF + (c + 1) * NT)
-                nc.vector.tensor_reduce(out=stats[:, i:i + 1], in_=o[m][:, cols], axis=AX.X, op=ALU.max,
-                                        apply_absolute_value=True)
+                abs_max(o[m][:, cols])
                 nc.sync.dma_start(out=out_0[m * P:(m + 1) * P, cols], in_=o[m][:, cols])
 
         for h in range(2):
-            left_amax(0, h)
-            left_widen(0, h)
-            left_store(0, h)
+            abs_max(xl0[h][:])
+            nc.scalar.copy(out=o[0][:, 1024 * h:1024 * (h + 1)], in_=xl0[h][:])
+        nc.sync.dma_start(out=out_0[0:P, 0:HALF], in_=o[0][:, 0:HALF])
         x_transpose(0, 0)
         x_transpose(0, 1)
         x_evac(0, 0)
         x_evac(0, 1)
+        abs_max(xl1[:])
         for h in range(2):
-            left_amax(1, h)
-            left_widen(1, h)
-            left_store(1, h)
+            nc.gpsimd.tensor_scalar(out=o[1][:, 1024 * h:1024 * (h + 1)], in0=xl1[:, 1024 * h:1024 * (h + 1)],
+                                    scalar1=1.0, scalar2=0.0, op0=ALU.mult, op1=ALU.add)
+        nc.sync.dma_start(out=out_0[P:B, 0:HALF], in_=o[1][:, 0:HALF])
         x_transpose(1, 0)
         x_transpose(1, 1)
         x_evac(1, 0)
-        x_quant(0, 0)
-        x_quant(0, 1)
+        x_quant(0)
 
-        n_units = len(units)
-        first_last = n_units - NCH
+        n_units = len(UNITS)
         for k in range(n_units + AMAX_LAG):
             if k < n_units:
                 interleave(k)
             if k == 0:
-                x_quant(1, 0)
                 x_evac(1, 1)
             if k == 1:
-                x_quant(1, 1)
+                x_quant(1)
             if 0 <= k - 1 < n_units:
                 quantize(k - 1)
                 multiply(k - 1)
-            if first_last <= k - EVAC_LAG < n_units:
-                right_evac(k - EVAC_LAG - first_last)
-            if first_last <= k - AMAX_LAG < n_units:
-                right_amax_store(k - AMAX_LAG - first_last)
+            if 0 <= k - EVAC_LAG < n_units and UNITS[k - EVAC_LAG][0] == PASSES - 1:
+                right_evac(k - EVAC_LAG)
+            if 0 <= k - AMAX_LAG < n_units and UNITS[k - AMAX_LAG][0] == PASSES - 1:
+                right_amax_store(k - AMAX_LAG)
+        assert n_used[0] == N_STATS
 
+        scaled = keep.tile([P, N_STATS], F32, name="scaled")
         part = keep.tile([P, 1], F32, name="part")
-        nc.vector.tensor_reduce(out=part[:], in_=stats[:], axis=AX.X, op=ALU.max)
+        nc.vector.tensor_scalar(out=scaled[:], in0=stats[:], scalar1=1.0 / 448.0, scalar2=None, op0=ALU.mult,
+                                op1=ALU.max, accum_out=part[:, 0:1])
         spread = psum.tile([P, P], F32, name="spread", tag="bank0")
         nc.tensor.transpose(spread[:], part[:, 0:1].to_broadcast([P, P]), ident[:])
-        amax = keep.tile([P, 1], F32, name="amax")
-        nc.vector.tensor_reduce(out=amax[:], in_=spread[:], axis=AX.X, op=ALU.max)
-        rinv = keep.tile([P, 1], F32, name="rinv")
-        nc.vector.reciprocal(out=rinv[:], in_=amax[:])
+        scale = keep.tile([P, 1], F32, name="scale")
+        nc.vector.tensor_reduce(out=scale[:], in_=spread[:], axis=AX.X, op=ALU.max)
         factor = keep.tile([P, 1], F32, name="factor")
-        nc.vector.tensor_scalar(out=factor[:], in0=rinv[:], scalar1=448.0, scalar2=None, op0=ALU.mult)
+        nc.vector.reciprocal(out=factor[:], in_=scale[:])
 
         for m, a, width in CAST_PIECES:
             vw = int(width * CAST_V_SHARE) // 16 * 16

@@ -26,13 +26,9 @@ MT = B // P
 FLOPS = 2 * B * HALF * HALF
 BYTES = B * DIM * 2 + HALF * HALF * 2 + B * DIM * 4 + B * DIM
 
-UNITS = (
-    (0, 0, 512, 352), (0, 512, 512, 240), (0, 1024, 1024, 528),
-    (1, 0, 1024, 512), (1, 1024, 1024, 512),
-    (2, 0, 1024, 496), (2, 1024, 1024, 480),
-    (3, 0, 1024, 480), (3, 1024, 512, 240), (3, 1536, 512, 288),
-)
-GROUPED_BUFS = 3
+V_COLS = 240
+GROUPED_BUFS = 4
+LOAD_WIDTHS = ((512, 512, 512, 512), (512, 512, 512, 512), (512, 512, 512, 512), (512, 512, 512, 512))
 EVAC_LAG = 2
 AMAX_LAG = 3
 CAST_PIECES = ((0, 0, 2048), (0, 2048, 2048), (1, 0, 2048), (1, 2048, 1024), (1, 3072, 1024))
@@ -54,164 +50,177 @@ def tile_builtcontrolled_kernel(tc, state, target_matrix, control, num_qubits, o
         warm = keep.tile([P, 1], F32, name="warm")
         nc.scalar.activation(out=warm[:], in_=zero[:], func=ACT.Identity, scale=zero[:, 0:1], bias=zero[:, 0:1])
 
-        xl0 = [keep.tile([P, 1024], BF16, name="xl0%d" % h) for h in range(2)]
-        xl1 = keep.tile([P, HALF], BF16, name="xl1")
-        xr = [keep.tile([P, HALF], BF16, name="xr%d" % m) for m in range(MT)]
-        for h in range(2):
-            nc.sync.dma_start(out=xl0[h][:], in_=state[0:P, 1024 * h:1024 * (h + 1)])
-        nc.sync.dma_start(out=xr[0][:], in_=state[0:P, HALF:DIM])
-        nc.sync.dma_start(out=xl1[:], in_=state[P:B, 0:HALF])
-        nc.sync.dma_start(out=xr[1][:], in_=state[P:B, HALF:DIM])
-        raws = []
-        for k, (g, c0, width, v_cols) in enumerate(UNITS):
-            raw = keep.tile([P, 4, width], BF16, name="raw%d" % k)
-            nc.sync.dma_start(
-                out=raw[:],
-                in_=target_matrix[HALF + K_PASS * g:HALF + K_PASS * (g + 1), HALF + c0:HALF + c0 + width]
-                .rearrange("(p j) w -> p j w", j=4),
-            )
-            raws.append(raw)
+        xl = {}
+        xr = {}
+        for m in range(MT):
+            rows = slice(m * P, (m + 1) * P)
+            for h in range(2):
+                xl[(m, h)] = keep.tile([P, 1024], BF16, name="xl%d%d" % (m, h))
+                nc.sync.dma_start(out=xl[(m, h)][:], in_=state[rows, 1024 * h:1024 * (h + 1)])
+            for h in range(2):
+                xr[(m, h)] = keep.tile([P, 1024], BF16, name="xr%d%d" % (m, h))
+                nc.sync.dma_start(out=xr[(m, h)][:], in_=state[rows, HALF + 1024 * h:HALF + 1024 * (h + 1)])
+        raw_of = {}
+        for g in range(PASSES):
+            c0 = 0
+            for d, width in enumerate(LOAD_WIDTHS[g]):
+                raw = keep.tile([P, 4, width], BF16, name="raw%d%d" % (g, d))
+                nc.sync.dma_start(
+                    out=raw[:],
+                    in_=target_matrix[HALF + K_PASS * g:HALF + K_PASS * (g + 1), HALF + c0:HALF + c0 + width]
+                    .rearrange("(p j) w -> p j w", j=4),
+                )
+                for c in range(c0 // NT, (c0 + width) // NT):
+                    raw_of[(g, c)] = (raw, c * NT - c0)
+                c0 += width
 
         t_codes = keep.tile([P, PASSES * HALF], U32, name="t_codes", align_bytes=64)
         t_scales = keep.tile([P, PASSES * HALF], U8, name="t_scales", align_bytes=64)
         x_codes = keep.tile([P, MT * PASSES * P], U32, name="x_codes", align_bytes=64)
         x_scales = keep.tile([P, MT * PASSES * P], U8, name="x_scales", align_bytes=64)
-        xg = [keep.tile([P, PASSES, P, 4], BF16, name="xg%d" % m, align_bytes=64) for m in range(MT)]
         o = [keep.tile([P, DIM], F32, name="o%d" % m) for m in range(MT)]
         q8 = [keep.tile([P, DIM], FP8, name="q8%d" % m) for m in range(MT)]
-        N_STATS = 9
-        stats = keep.tile([P, N_STATS], F32, name="stats")
-        n_used = [0]
+        n_stats = 4 + MT * NCH
+        stats = keep.tile([P, n_stats], F32, name="stats")
 
-        def abs_max(src):
-            i = n_used[0]
-            n_used[0] = i + 1
-            nc.vector.tensor_reduce(out=stats[:, i:i + 1], in_=src, axis=AX.X, op=ALU.max, apply_absolute_value=True)
+        def left_amax(m, h):
+            i = 2 * m + h
+            nc.vector.tensor_reduce(out=stats[:, i:i + 1], in_=xl[(m, h)][:], axis=AX.X, op=ALU.max,
+                                    apply_absolute_value=True)
+
+        def left_widen(m, h):
+            dst = o[m][:, 1024 * h:1024 * (h + 1)]
+            if m == 0:
+                nc.scalar.copy(out=dst, in_=xl[(m, h)][:])
+            else:
+                nc.gpsimd.tensor_scalar(out=dst, in0=xl[(m, h)][:], scalar1=1.0, scalar2=0.0,
+                                        op0=ALU.mult, op1=ALU.add)
+
+        def left_store(m, h):
+            nc.sync.dma_start(out=out_0[m * P:(m + 1) * P, 1024 * h:1024 * (h + 1)],
+                              in_=o[m][:, 1024 * h:1024 * (h + 1)])
 
         xt = {}
+        xg = {}
         XT_BANK = {(0, 0): 2, (0, 1): 3, (1, 0): 6, (1, 1): 7}
 
         def x_transpose(m, h):
-            words = xr[m][:].bitcast(F32)
+            words = xr[(m, h)][:].bitcast(F32)
             xt[(m, h)] = psum.tile([P, 2, 2, P], F32, name="xt%d%d" % (m, h), tag="bank%d" % XT_BANK[(m, h)])
             for gi in range(2):
-                g = 2 * h + gi
                 for u in range(2):
-                    nc.tensor.transpose(xt[(m, h)][:, gi, u, :], words[:, 256 * g + u:256 * (g + 1):2], ident[:])
+                    nc.tensor.transpose(xt[(m, h)][:, gi, u, :], words[:, 256 * gi + u:256 * (gi + 1):2], ident[:])
 
         def x_evac(m, h):
-            nc.scalar.copy(out=xg[m][:, 2 * h:2 * h + 2, :, :].bitcast(F32),
-                           in_=xt[(m, h)][:].rearrange("p g u r -> p g r u"))
+            xg[(m, h)] = keep.tile([P, 2, P, 4], BF16, name="xg%d%d" % (m, h), align_bytes=64)
+            nc.scalar.copy(out=xg[(m, h)][:].bitcast(F32), in_=xt[(m, h)][:].rearrange("p g u r -> p g r u"))
 
-        def x_quant(m):
-            base = m * PASSES * P
+        def x_quant(m, h):
+            base = (m * PASSES + 2 * h) * P
             nc.vector.quantize_mx(
-                out=x_codes[:, base:base + PASSES * P].bitcast(FP8X4),
-                scales=x_scales[:, base:base + PASSES * P],
-                in_=xg[m][:].rearrange("p g r j -> p (g r j)"),
+                out=x_codes[:, base:base + 2 * P].bitcast(FP8X4),
+                scales=x_scales[:, base:base + 2 * P],
+                in_=xg[(m, h)][:].rearrange("p g r j -> p (g r j)"),
             )
 
+        units = [(g, c) for g in range(PASSES) for c in range(NCH)]
         grouped = {}
         acc = {}
 
         def interleave(k):
-            g, c0, width, v_cols = UNITS[k]
-            raw = raws[k]
-            grp = stage.tile([P, width, 4], BF16, name="grp", align_bytes=64)
+            g, c = units[k]
+            raw, c0 = raw_of[(g, c)]
+            grp = stage.tile([P, NT, 4], BF16, name="grp", align_bytes=64)
             grouped[k] = grp
-            nc.vector.tensor_copy(out=grp[:, 0:v_cols, :].rearrange("p (c i) t -> p c t i", i=4),
-                                  in_=raw[:, :, 0:v_cols].rearrange("p t (c i) -> p c t i", i=4))
-            nc.scalar.copy(out=grp[:, v_cols:width, :].rearrange("p (c i) t -> p c t i", i=4),
-                           in_=raw[:, :, v_cols:width].rearrange("p t (c i) -> p c t i", i=4))
+            nc.vector.tensor_copy(out=grp[:, 0:V_COLS, :].rearrange("p (c i) t -> p c t i", i=4),
+                                  in_=raw[:, :, c0:c0 + V_COLS].rearrange("p t (c i) -> p c t i", i=4))
+            nc.scalar.copy(out=grp[:, V_COLS:NT, :].rearrange("p (c i) t -> p c t i", i=4),
+                           in_=raw[:, :, c0 + V_COLS:c0 + NT].rearrange("p t (c i) -> p c t i", i=4))
 
         def quantize(k):
-            g, c0, width, v_cols = UNITS[k]
-            tb = g * HALF + c0
+            g, c = units[k]
+            tb = g * HALF + c * NT
             nc.vector.quantize_mx(
-                out=t_codes[:, tb:tb + width].bitcast(FP8X4),
-                scales=t_scales[:, tb:tb + width],
+                out=t_codes[:, tb:tb + NT].bitcast(FP8X4),
+                scales=t_scales[:, tb:tb + NT],
                 in_=grouped[k][:].rearrange("p w j -> p (w j)"),
             )
 
         def multiply(k):
-            g, c0, width, v_cols = UNITS[k]
-            for c in range(c0 // NT, (c0 + width) // NT):
-                tb = g * HALF + c * NT
-                for m in range(MT):
-                    if g == 0:
-                        acc[(m, c)] = psum.tile([P, NT], F32, name="acc%d%d" % (m, c), tag="bank%d" % (NCH * m + c))
-                    xb = (m * PASSES + g) * P
-                    nc.tensor.matmul_mx(
-                        out=acc[(m, c)][:],
-                        lhsT=x_codes[:, xb:xb + P].bitcast(FP8X4),
-                        lhsT_scale=x_scales[:, xb:xb + P],
-                        rhs=t_codes[:, tb:tb + NT].bitcast(FP8X4),
-                        rhs_scale=t_scales[:, tb:tb + NT],
-                        start=(g == 0),
-                        stop=(g == PASSES - 1),
-                    )
-
-        def right_evac(k):
-            g, c0, width, v_cols = UNITS[k]
+            g, c = units[k]
+            tb = g * HALF + c * NT
             for m in range(MT):
-                for c in range(c0 // NT, (c0 + width) // NT):
-                    nc.scalar.copy(out=o[m][:, HALF + c * NT:HALF + (c + 1) * NT], in_=acc[(m, c)][:])
-                    if (m, c) != (0, 0):
-                        busy = psum.tile([P, NT], F32, name="busy%d%d" % (m, c), tag="bank%d" % (NCH * m + c))
-                        nc.tensor.matmul(out=busy[:], lhsT=xl0[0][:, 0:P], rhs=xl0[0][:, 0:NT], start=True, stop=True)
+                if g == 0:
+                    acc[(m, c)] = psum.tile([P, NT], F32, name="acc%d%d" % (m, c), tag="bank%d" % (NCH * m + c))
+                xb = (m * PASSES + g) * P
+                nc.tensor.matmul_mx(
+                    out=acc[(m, c)][:],
+                    lhsT=x_codes[:, xb:xb + P].bitcast(FP8X4),
+                    lhsT_scale=x_scales[:, xb:xb + P],
+                    rhs=t_codes[:, tb:tb + NT].bitcast(FP8X4),
+                    rhs_scale=t_scales[:, tb:tb + NT],
+                    start=(g == 0),
+                    stop=(g == PASSES - 1),
+                )
 
-        def right_amax_store(k):
-            g, c0, width, v_cols = UNITS[k]
-            cols = slice(HALF + c0, HALF + c0 + width)
+        def right_evac(c):
             for m in range(MT):
-                abs_max(o[m][:, cols])
+                nc.scalar.copy(out=o[m][:, HALF + c * NT:HALF + (c + 1) * NT], in_=acc[(m, c)][:])
+
+        def right_amax_store(c):
+            for m in range(MT):
+                i = 4 + NCH * m + c
+                cols = slice(HALF + c * NT, HALF + (c + 1) * NT)
+                nc.vector.tensor_reduce(out=stats[:, i:i + 1], in_=o[m][:, cols], axis=AX.X, op=ALU.max,
+                                        apply_absolute_value=True)
                 nc.sync.dma_start(out=out_0[m * P:(m + 1) * P, cols], in_=o[m][:, cols])
 
         for h in range(2):
-            abs_max(xl0[h][:])
-            nc.scalar.copy(out=o[0][:, 1024 * h:1024 * (h + 1)], in_=xl0[h][:])
-        nc.sync.dma_start(out=out_0[0:P, 0:HALF], in_=o[0][:, 0:HALF])
+            left_amax(0, h)
+            left_widen(0, h)
+            left_store(0, h)
         x_transpose(0, 0)
         x_transpose(0, 1)
         x_evac(0, 0)
         x_evac(0, 1)
-        abs_max(xl1[:])
         for h in range(2):
-            nc.gpsimd.tensor_scalar(out=o[1][:, 1024 * h:1024 * (h + 1)], in0=xl1[:, 1024 * h:1024 * (h + 1)],
-                                    scalar1=1.0, scalar2=0.0, op0=ALU.mult, op1=ALU.add)
-        nc.sync.dma_start(out=out_0[P:B, 0:HALF], in_=o[1][:, 0:HALF])
+            left_amax(1, h)
+            left_widen(1, h)
+            left_store(1, h)
         x_transpose(1, 0)
         x_transpose(1, 1)
         x_evac(1, 0)
-        x_quant(0)
+        x_quant(0, 0)
+        x_quant(0, 1)
 
-        n_units = len(UNITS)
+        n_units = len(units)
+        first_last = n_units - NCH
         for k in range(n_units + AMAX_LAG):
             if k < n_units:
                 interleave(k)
             if k == 0:
+                x_quant(1, 0)
                 x_evac(1, 1)
             if k == 1:
-                x_quant(1)
+                x_quant(1, 1)
             if 0 <= k - 1 < n_units:
                 quantize(k - 1)
                 multiply(k - 1)
-            if 0 <= k - EVAC_LAG < n_units and UNITS[k - EVAC_LAG][0] == PASSES - 1:
-                right_evac(k - EVAC_LAG)
-            if 0 <= k - AMAX_LAG < n_units and UNITS[k - AMAX_LAG][0] == PASSES - 1:
-                right_amax_store(k - AMAX_LAG)
-        assert n_used[0] == N_STATS
+            if first_last <= k - EVAC_LAG < n_units:
+                right_evac(k - EVAC_LAG - first_last)
+            if first_last <= k - AMAX_LAG < n_units:
+                right_amax_store(k - AMAX_LAG - first_last)
 
-        scaled = keep.tile([P, N_STATS], F32, name="scaled")
         part = keep.tile([P, 1], F32, name="part")
-        nc.vector.tensor_scalar(out=scaled[:], in0=stats[:], scalar1=1.0 / 448.0, scalar2=None, op0=ALU.mult,
-                                op1=ALU.max, accum_out=part[:, 0:1])
+        nc.vector.tensor_reduce(out=part[:], in_=stats[:], axis=AX.X, op=ALU.max)
         spread = psum.tile([P, P], F32, name="spread", tag="bank0")
         nc.tensor.transpose(spread[:], part[:, 0:1].to_broadcast([P, P]), ident[:])
-        scale = keep.tile([P, 1], F32, name="scale")
-        nc.vector.tensor_reduce(out=scale[:], in_=spread[:], axis=AX.X, op=ALU.max)
+        amax = keep.tile([P, 1], F32, name="amax")
+        nc.vector.tensor_reduce(out=amax[:], in_=spread[:], axis=AX.X, op=ALU.max)
+        rinv = keep.tile([P, 1], F32, name="rinv")
+        nc.vector.reciprocal(out=rinv[:], in_=amax[:])
         factor = keep.tile([P, 1], F32, name="factor")
-        nc.vector.reciprocal(out=factor[:], in_=scale[:])
+        nc.vector.tensor_scalar(out=factor[:], in0=rinv[:], scalar1=448.0, scalar2=None, op0=ALU.mult)
 
         for m, a, width in CAST_PIECES:
             vw = int(width * CAST_V_SHARE) // 16 * 16

@@ -14,23 +14,27 @@ ACT = mybir.ActivationFunctionType
 AX = mybir.AxisListType
 
 P = 128
-B = 256
+ROWS = 256
 DIM = 4096
 HALF = 2048
-PASSES = 4
-K_PASS = 512
-NT = 512
-NCH = HALF // NT
-MT = B // P
+PACK = 4
+K_PASS = P * PACK
+PASSES = HALF // K_PASS
+ROW_TILES = ROWS // P
+BANK = 512
+BANKS = HALF // BANK
+PIECE = 1024
+PIECES = HALF // PIECE
 
-FLOPS = 2 * B * HALF * HALF
-BYTES = B * DIM * 2 + HALF * HALF * 2 + B * DIM * 4 + B * DIM
+FLOPS = 2 * ROWS * HALF * HALF
+BYTES = ROWS * DIM * 2 + HALF * HALF * 2 + ROWS * DIM * 4 + ROWS * DIM
 
+LOAD_WIDTHS = ((512, 512, 1024), (1024, 1024), (1024, 1024), (1024, 1024))
 V_COLS = 240
 GROUPED_BUFS = 4
-LOAD_WIDTHS = ((512, 512, 512, 512), (512, 512, 512, 512), (512, 512, 512, 512), (512, 512, 512, 512))
 EVAC_LAG = 2
 AMAX_LAG = 3
+XT_BANK = {(0, 0): 2, (0, 1): 3, (1, 0): 6, (1, 1): 7}
 CAST_PIECES = ((0, 0, 2048), (0, 2048, 2048), (1, 0, 2048), (1, 2048, 1024), (1, 3072, 1024))
 CAST_V_SHARE = 0.67
 
@@ -50,143 +54,135 @@ def tile_builtcontrolled_kernel(tc, state, target_matrix, control, num_qubits, o
         warm = keep.tile([P, 1], F32, name="warm")
         nc.scalar.activation(out=warm[:], in_=zero[:], func=ACT.Identity, scale=zero[:, 0:1], bias=zero[:, 0:1])
 
-        xl = {}
-        xr = {}
-        for m in range(MT):
+        left = {}
+        right = {}
+        for m in range(ROW_TILES):
             rows = slice(m * P, (m + 1) * P)
-            for h in range(2):
-                xl[(m, h)] = keep.tile([P, 1024], BF16, name="xl%d%d" % (m, h))
-                nc.sync.dma_start(out=xl[(m, h)][:], in_=state[rows, 1024 * h:1024 * (h + 1)])
-            for h in range(2):
-                xr[(m, h)] = keep.tile([P, 1024], BF16, name="xr%d%d" % (m, h))
-                nc.sync.dma_start(out=xr[(m, h)][:], in_=state[rows, HALF + 1024 * h:HALF + 1024 * (h + 1)])
+            for h in range(PIECES):
+                left[(m, h)] = keep.tile([P, PIECE], BF16, name="xl%d%d" % (m, h))
+                nc.sync.dma_start(out=left[(m, h)][:], in_=state[rows, PIECE * h:PIECE * (h + 1)])
+            for h in range(PIECES):
+                right[(m, h)] = keep.tile([P, PIECE], BF16, name="xr%d%d" % (m, h))
+                nc.sync.dma_start(out=right[(m, h)][:], in_=state[rows, HALF + PIECE * h:HALF + PIECE * (h + 1)])
         raw_of = {}
         for g in range(PASSES):
             c0 = 0
             for d, width in enumerate(LOAD_WIDTHS[g]):
-                raw = keep.tile([P, 4, width], BF16, name="raw%d%d" % (g, d))
+                raw = keep.tile([P, PACK, width], BF16, name="raw%d%d" % (g, d))
                 nc.sync.dma_start(
                     out=raw[:],
                     in_=target_matrix[HALF + K_PASS * g:HALF + K_PASS * (g + 1), HALF + c0:HALF + c0 + width]
-                    .rearrange("(p j) w -> p j w", j=4),
+                    .rearrange("(p t) w -> p t w", t=PACK),
                 )
-                for c in range(c0 // NT, (c0 + width) // NT):
-                    raw_of[(g, c)] = (raw, c * NT - c0)
+                for c in range(c0 // BANK, (c0 + width) // BANK):
+                    raw_of[(g, c)] = (raw, c * BANK - c0)
                 c0 += width
 
         t_codes = keep.tile([P, PASSES * HALF], U32, name="t_codes", align_bytes=64)
         t_scales = keep.tile([P, PASSES * HALF], U8, name="t_scales", align_bytes=64)
-        x_codes = keep.tile([P, MT * PASSES * P], U32, name="x_codes", align_bytes=64)
-        x_scales = keep.tile([P, MT * PASSES * P], U8, name="x_scales", align_bytes=64)
-        o = [keep.tile([P, DIM], F32, name="o%d" % m) for m in range(MT)]
-        q8 = [keep.tile([P, DIM], FP8, name="q8%d" % m) for m in range(MT)]
-        n_stats = 4 + MT * NCH
+        x_codes = keep.tile([P, ROW_TILES * PASSES * P], U32, name="x_codes", align_bytes=64)
+        x_scales = keep.tile([P, ROW_TILES * PASSES * P], U8, name="x_scales", align_bytes=64)
+        o = [keep.tile([P, DIM], F32, name="o%d" % m) for m in range(ROW_TILES)]
+        o8 = [keep.tile([P, DIM], FP8, name="q8%d" % m) for m in range(ROW_TILES)]
+        n_stats = ROW_TILES * (PIECES + BANKS)
         stats = keep.tile([P, n_stats], F32, name="stats")
 
-        def left_amax(m, h):
-            i = 2 * m + h
-            nc.vector.tensor_reduce(out=stats[:, i:i + 1], in_=xl[(m, h)][:], axis=AX.X, op=ALU.max,
-                                    apply_absolute_value=True)
+        def abs_max(i, src):
+            nc.vector.tensor_reduce(out=stats[:, i:i + 1], in_=src, axis=AX.X, op=ALU.max, apply_absolute_value=True)
 
-        def left_widen(m, h):
-            dst = o[m][:, 1024 * h:1024 * (h + 1)]
+        def left_half(m, h):
+            cols = slice(PIECE * h, PIECE * (h + 1))
+            abs_max(PIECES * m + h, left[(m, h)][:])
             if m == 0:
-                nc.scalar.copy(out=dst, in_=xl[(m, h)][:])
+                nc.scalar.copy(out=o[m][:, cols], in_=left[(m, h)][:])
             else:
-                nc.gpsimd.tensor_scalar(out=dst, in0=xl[(m, h)][:], scalar1=1.0, scalar2=0.0,
+                nc.gpsimd.tensor_scalar(out=o[m][:, cols], in0=left[(m, h)][:], scalar1=1.0, scalar2=0.0,
                                         op0=ALU.mult, op1=ALU.add)
-
-        def left_store(m, h):
-            nc.sync.dma_start(out=out_0[m * P:(m + 1) * P, 1024 * h:1024 * (h + 1)],
-                              in_=o[m][:, 1024 * h:1024 * (h + 1)])
+            nc.sync.dma_start(out=out_0[m * P:(m + 1) * P, cols], in_=o[m][:, cols])
 
         xt = {}
-        xg = {}
-        XT_BANK = {(0, 0): 2, (0, 1): 3, (1, 0): 6, (1, 1): 7}
+        x_grouped = {}
 
         def x_transpose(m, h):
-            words = xr[(m, h)][:].bitcast(F32)
+            words = right[(m, h)][:].bitcast(F32)
             xt[(m, h)] = psum.tile([P, 2, 2, P], F32, name="xt%d%d" % (m, h), tag="bank%d" % XT_BANK[(m, h)])
             for gi in range(2):
                 for u in range(2):
                     nc.tensor.transpose(xt[(m, h)][:, gi, u, :], words[:, 256 * gi + u:256 * (gi + 1):2], ident[:])
 
         def x_evac(m, h):
-            xg[(m, h)] = keep.tile([P, 2, P, 4], BF16, name="xg%d%d" % (m, h), align_bytes=64)
-            nc.scalar.copy(out=xg[(m, h)][:].bitcast(F32), in_=xt[(m, h)][:].rearrange("p g u r -> p g r u"))
+            x_grouped[(m, h)] = keep.tile([P, 2, P, PACK], BF16, name="xg%d%d" % (m, h), align_bytes=64)
+            nc.scalar.copy(out=x_grouped[(m, h)][:].bitcast(F32), in_=xt[(m, h)][:].rearrange("p g u r -> p g r u"))
 
         def x_quant(m, h):
             base = (m * PASSES + 2 * h) * P
             nc.vector.quantize_mx(
                 out=x_codes[:, base:base + 2 * P].bitcast(FP8X4),
                 scales=x_scales[:, base:base + 2 * P],
-                in_=xg[(m, h)][:].rearrange("p g r j -> p (g r j)"),
+                in_=x_grouped[(m, h)][:].rearrange("p g r t -> p (g r t)"),
             )
 
-        units = [(g, c) for g in range(PASSES) for c in range(NCH)]
+        units = [(g, c) for g in range(PASSES) for c in range(BANKS)]
         grouped = {}
         acc = {}
 
         def interleave(k):
-            g, c = units[k]
-            raw, c0 = raw_of[(g, c)]
-            grp = stage.tile([P, NT, 4], BF16, name="grp", align_bytes=64)
+            raw, c0 = raw_of[units[k]]
+            grp = stage.tile([P, BANK, PACK], BF16, name="grp", align_bytes=64)
             grouped[k] = grp
             nc.vector.tensor_copy(out=grp[:, 0:V_COLS, :].rearrange("p (c i) t -> p c t i", i=4),
                                   in_=raw[:, :, c0:c0 + V_COLS].rearrange("p t (c i) -> p c t i", i=4))
-            nc.scalar.copy(out=grp[:, V_COLS:NT, :].rearrange("p (c i) t -> p c t i", i=4),
-                           in_=raw[:, :, c0 + V_COLS:c0 + NT].rearrange("p t (c i) -> p c t i", i=4))
+            nc.scalar.copy(out=grp[:, V_COLS:BANK, :].rearrange("p (c i) t -> p c t i", i=4),
+                           in_=raw[:, :, c0 + V_COLS:c0 + BANK].rearrange("p t (c i) -> p c t i", i=4))
 
         def quantize(k):
             g, c = units[k]
-            tb = g * HALF + c * NT
+            tb = g * HALF + c * BANK
             nc.vector.quantize_mx(
-                out=t_codes[:, tb:tb + NT].bitcast(FP8X4),
-                scales=t_scales[:, tb:tb + NT],
-                in_=grouped[k][:].rearrange("p w j -> p (w j)"),
+                out=t_codes[:, tb:tb + BANK].bitcast(FP8X4),
+                scales=t_scales[:, tb:tb + BANK],
+                in_=grouped[k][:].rearrange("p w t -> p (w t)"),
             )
 
         def multiply(k):
             g, c = units[k]
-            tb = g * HALF + c * NT
-            for m in range(MT):
+            tb = g * HALF + c * BANK
+            for m in range(ROW_TILES):
                 if g == 0:
-                    acc[(m, c)] = psum.tile([P, NT], F32, name="acc%d%d" % (m, c), tag="bank%d" % (NCH * m + c))
+                    acc[(m, c)] = psum.tile([P, BANK], F32, name="acc%d%d" % (m, c), tag="bank%d" % (BANKS * m + c))
                 xb = (m * PASSES + g) * P
                 nc.tensor.matmul_mx(
                     out=acc[(m, c)][:],
                     lhsT=x_codes[:, xb:xb + P].bitcast(FP8X4),
                     lhsT_scale=x_scales[:, xb:xb + P],
-                    rhs=t_codes[:, tb:tb + NT].bitcast(FP8X4),
-                    rhs_scale=t_scales[:, tb:tb + NT],
+                    rhs=t_codes[:, tb:tb + BANK].bitcast(FP8X4),
+                    rhs_scale=t_scales[:, tb:tb + BANK],
                     start=(g == 0),
                     stop=(g == PASSES - 1),
                 )
 
         def right_evac(c):
-            for m in range(MT):
-                nc.scalar.copy(out=o[m][:, HALF + c * NT:HALF + (c + 1) * NT], in_=acc[(m, c)][:])
+            for m in range(ROW_TILES):
+                nc.scalar.copy(out=o[m][:, HALF + c * BANK:HALF + (c + 1) * BANK], in_=acc[(m, c)][:])
+                if c >= BANKS - 2:
+                    busy = psum.tile([P, BANK], F32, name="busy%d%d" % (m, c), tag="bank%d" % (BANKS * m + c))
+                    nc.tensor.matmul(out=busy[:], lhsT=left[(0, 0)][:, 0:P], rhs=left[(0, 0)][:, 0:BANK],
+                                     start=True, stop=True)
 
         def right_amax_store(c):
-            for m in range(MT):
-                i = 4 + NCH * m + c
-                cols = slice(HALF + c * NT, HALF + (c + 1) * NT)
-                nc.vector.tensor_reduce(out=stats[:, i:i + 1], in_=o[m][:, cols], axis=AX.X, op=ALU.max,
-                                        apply_absolute_value=True)
+            cols = slice(HALF + c * BANK, HALF + (c + 1) * BANK)
+            for m in range(ROW_TILES):
+                abs_max(ROW_TILES * PIECES + BANKS * m + c, o[m][:, cols])
                 nc.sync.dma_start(out=out_0[m * P:(m + 1) * P, cols], in_=o[m][:, cols])
 
-        for h in range(2):
-            left_amax(0, h)
-            left_widen(0, h)
-            left_store(0, h)
+        for h in range(PIECES):
+            left_half(0, h)
         x_transpose(0, 0)
         x_transpose(0, 1)
         x_evac(0, 0)
         x_evac(0, 1)
-        for h in range(2):
-            left_amax(1, h)
-            left_widen(1, h)
-            left_store(1, h)
+        for h in range(PIECES):
+            left_half(1, h)
         x_transpose(1, 0)
         x_transpose(1, 1)
         x_evac(1, 0)
@@ -194,7 +190,7 @@ def tile_builtcontrolled_kernel(tc, state, target_matrix, control, num_qubits, o
         x_quant(0, 1)
 
         n_units = len(units)
-        first_last = n_units - NCH
+        first_of_last_pass = n_units - BANKS
         for k in range(n_units + AMAX_LAG):
             if k < n_units:
                 interleave(k)
@@ -206,26 +202,26 @@ def tile_builtcontrolled_kernel(tc, state, target_matrix, control, num_qubits, o
             if 0 <= k - 1 < n_units:
                 quantize(k - 1)
                 multiply(k - 1)
-            if first_last <= k - EVAC_LAG < n_units:
-                right_evac(k - EVAC_LAG - first_last)
-            if first_last <= k - AMAX_LAG < n_units:
-                right_amax_store(k - AMAX_LAG - first_last)
+            if 0 <= k - EVAC_LAG - first_of_last_pass < BANKS:
+                right_evac(k - EVAC_LAG - first_of_last_pass)
+            if 0 <= k - AMAX_LAG - first_of_last_pass < BANKS:
+                right_amax_store(k - AMAX_LAG - first_of_last_pass)
 
+        scaled = keep.tile([P, n_stats], F32, name="scaled")
         part = keep.tile([P, 1], F32, name="part")
-        nc.vector.tensor_reduce(out=part[:], in_=stats[:], axis=AX.X, op=ALU.max)
+        nc.vector.tensor_scalar(out=scaled[:], in0=stats[:], scalar1=1.0 / 448.0, scalar2=None, op0=ALU.mult,
+                                op1=ALU.max, accum_out=part[:, 0:1])
         spread = psum.tile([P, P], F32, name="spread", tag="bank0")
         nc.tensor.transpose(spread[:], part[:, 0:1].to_broadcast([P, P]), ident[:])
-        amax = keep.tile([P, 1], F32, name="amax")
-        nc.vector.tensor_reduce(out=amax[:], in_=spread[:], axis=AX.X, op=ALU.max)
-        rinv = keep.tile([P, 1], F32, name="rinv")
-        nc.vector.reciprocal(out=rinv[:], in_=amax[:])
+        scale = keep.tile([P, 1], F32, name="scale")
+        nc.vector.tensor_reduce(out=scale[:], in_=spread[:], axis=AX.X, op=ALU.max)
         factor = keep.tile([P, 1], F32, name="factor")
-        nc.vector.tensor_scalar(out=factor[:], in0=rinv[:], scalar1=448.0, scalar2=None, op0=ALU.mult)
+        nc.vector.reciprocal(out=factor[:], in_=scale[:])
 
         for m, a, width in CAST_PIECES:
             vw = int(width * CAST_V_SHARE) // 16 * 16
-            nc.vector.tensor_scalar(out=q8[m][:, a:a + vw], in0=o[m][:, a:a + vw], scalar1=factor[:, 0:1],
+            nc.vector.tensor_scalar(out=o8[m][:, a:a + vw], in0=o[m][:, a:a + vw], scalar1=factor[:, 0:1],
                                     scalar2=None, op0=ALU.mult, saturate=False)
-            nc.scalar.activation(out=q8[m][:, a + vw:a + width], in_=o[m][:, a + vw:a + width], func=ACT.Identity,
+            nc.scalar.activation(out=o8[m][:, a + vw:a + width], in_=o[m][:, a + vw:a + width], func=ACT.Identity,
                                  scale=factor[:, 0:1], bias=zero[:, 0:1], saturate=False)
-            nc.sync.dma_start(out=out_1[m * P:(m + 1) * P, a:a + width], in_=q8[m][:, a:a + width].bitcast(U8))
+            nc.sync.dma_start(out=out_1[m * P:(m + 1) * P, a:a + width], in_=o8[m][:, a:a + width].bitcast(U8))

@@ -29,7 +29,7 @@ PIECES = HALF // PIECE
 FLOPS = 2 * ROWS * HALF * HALF
 BYTES = ROWS * DIM * 2 + HALF * HALF * 2 + ROWS * DIM * 4 + ROWS * DIM
 
-LOAD_WIDTHS = ((512, 512, 1024), (1024, 1024), (1024, 1024), (1024, 1024))
+LOAD_WIDTHS = ((512, 512, 1024), (1024, 1024), (1024, 1024), (512, 512, 512, 512))
 V_COLS = 240
 GROUPED_BUFS = 4
 EVAC_LAG = 2
@@ -58,12 +58,13 @@ def tile_builtcontrolled_kernel(tc, state, target_matrix, control, num_qubits, o
         right = {}
         for m in range(ROW_TILES):
             rows = slice(m * P, (m + 1) * P)
+            xl = keep.tile([P, HALF], BF16, name="xl%d" % m)
+            nc.sync.dma_start(out=xl[:], in_=state[rows, 0:HALF])
+            xr = keep.tile([P, HALF], BF16, name="xr%d" % m)
+            nc.sync.dma_start(out=xr[:], in_=state[rows, HALF:DIM])
             for h in range(PIECES):
-                left[(m, h)] = keep.tile([P, PIECE], BF16, name="xl%d%d" % (m, h))
-                nc.sync.dma_start(out=left[(m, h)][:], in_=state[rows, PIECE * h:PIECE * (h + 1)])
-            for h in range(PIECES):
-                right[(m, h)] = keep.tile([P, PIECE], BF16, name="xr%d%d" % (m, h))
-                nc.sync.dma_start(out=right[(m, h)][:], in_=state[rows, HALF + PIECE * h:HALF + PIECE * (h + 1)])
+                left[(m, h)] = xl[:, PIECE * h:PIECE * (h + 1)]
+                right[(m, h)] = xr[:, PIECE * h:PIECE * (h + 1)]
         raw_of = {}
         for g in range(PASSES):
             c0 = 0
@@ -92,11 +93,11 @@ def tile_builtcontrolled_kernel(tc, state, target_matrix, control, num_qubits, o
 
         def left_half(m, h):
             cols = slice(PIECE * h, PIECE * (h + 1))
-            abs_max(PIECES * m + h, left[(m, h)][:])
+            abs_max(PIECES * m + h, left[(m, h)])
             if m == 0:
-                nc.scalar.copy(out=o[m][:, cols], in_=left[(m, h)][:])
+                nc.scalar.copy(out=o[m][:, cols], in_=left[(m, h)])
             else:
-                nc.gpsimd.tensor_scalar(out=o[m][:, cols], in0=left[(m, h)][:], scalar1=1.0, scalar2=0.0,
+                nc.gpsimd.tensor_scalar(out=o[m][:, cols], in0=left[(m, h)], scalar1=1.0, scalar2=0.0,
                                         op0=ALU.mult, op1=ALU.add)
             nc.sync.dma_start(out=out_0[m * P:(m + 1) * P, cols], in_=o[m][:, cols])
 
@@ -104,7 +105,7 @@ def tile_builtcontrolled_kernel(tc, state, target_matrix, control, num_qubits, o
         x_grouped = {}
 
         def x_transpose(m, h):
-            words = right[(m, h)][:].bitcast(F32)
+            words = right[(m, h)].bitcast(F32)
             xt[(m, h)] = psum.tile([P, 2, 2, P], F32, name="xt%d%d" % (m, h), tag="bank%d" % XT_BANK[(m, h)])
             for gi in range(2):
                 for u in range(2):

@@ -31,6 +31,10 @@ BYTES = ROWS * DIM * 2 + HALF * HALF * 2 + ROWS * DIM * 4 + ROWS * DIM
 
 LOAD_WIDTHS = ((512, 512, 1024), (1024, 1024), (1024, 1024), (512, 512, 512, 512))
 V_COLS = 240
+CHUNK_UNITS = (3, 5, 7, 9, 11)
+CHUNK_COLS = 256
+CHUNK_V_COLS = 176
+CHUNK_BANKS = (3, 7)
 GROUPED_BUFS = 4
 EVAC_LAG = 2
 AMAX_LAG = 3
@@ -49,6 +53,8 @@ def tile_builtcontrolled_kernel(tc, state, target_matrix, control, num_qubits, o
 
         ident = keep.tile([P, P], F32, name="ident")
         make_identity(nc, ident[:])
+        ident_bf = keep.tile([P, P], BF16, name="ident_bf")
+        make_identity(nc, ident_bf[:])
         zero = keep.tile([P, 1], F32, name="zero")
         nc.vector.memset(zero[:], 0.0)
         warm = keep.tile([P, 1], F32, name="warm")
@@ -131,10 +137,27 @@ def tile_builtcontrolled_kernel(tc, state, target_matrix, control, num_qubits, o
             raw, c0 = raw_of[units[k]]
             grp = stage.tile([P, BANK, PACK], BF16, name="grp", align_bytes=64)
             grouped[k] = grp
-            nc.vector.tensor_copy(out=grp[:, 0:V_COLS, :].rearrange("p (c i) t -> p c t i", i=4),
-                                  in_=raw[:, :, c0:c0 + V_COLS].rearrange("p t (c i) -> p c t i", i=4))
-            nc.scalar.copy(out=grp[:, V_COLS:BANK, :].rearrange("p (c i) t -> p c t i", i=4),
-                           in_=raw[:, :, c0 + V_COLS:c0 + BANK].rearrange("p t (c i) -> p c t i", i=4))
+            v_end = CHUNK_V_COLS if k in CHUNK_UNITS else V_COLS
+            s_end = BANK - CHUNK_COLS if k in CHUNK_UNITS else BANK
+            nc.vector.tensor_copy(out=grp[:, 0:v_end, :].rearrange("p (c i) t -> p c t i", i=4),
+                                  in_=raw[:, :, c0:c0 + v_end].rearrange("p t (c i) -> p c t i", i=4))
+            nc.scalar.copy(out=grp[:, v_end:s_end, :].rearrange("p (c i) t -> p c t i", i=4),
+                           in_=raw[:, :, c0 + v_end:c0 + s_end].rearrange("p t (c i) -> p c t i", i=4))
+            if k in CHUNK_UNITS:
+                nc.scalar.copy(out=grp[:, s_end:BANK, :].rearrange("p w t -> p (w t)"), in_=chunk[k][:])
+
+        chunk = {}
+
+        def tensor_interleave(k):
+            raw, c0 = raw_of[units[k]]
+            first = c0 + BANK - CHUNK_COLS
+            chunk[k] = psum.tile([P, CHUNK_COLS * PACK], BF16, name="chunk%d" % k,
+                                 tag="bank%d" % CHUNK_BANKS[CHUNK_UNITS.index(k) % len(CHUNK_BANKS)])
+            for j in range(CHUNK_COLS // P):
+                nc.tensor.matmul(out=chunk[k][:, BANK * j:BANK * (j + 1)].rearrange("p (w t) -> p w t", t=PACK),
+                                 lhsT=ident_bf[:],
+                                 rhs=raw[:, :, first + P * j:first + P * (j + 1)].rearrange("p t w -> p w t"),
+                                 start=True, stop=True)
 
         def quantize(k):
             g, c = units[k]
@@ -165,7 +188,7 @@ def tile_builtcontrolled_kernel(tc, state, target_matrix, control, num_qubits, o
         def right_evac(c):
             for m in range(ROW_TILES):
                 nc.scalar.copy(out=o[m][:, HALF + c * BANK:HALF + (c + 1) * BANK], in_=acc[(m, c)][:])
-                if c >= BANKS - 2:
+                if c >= BANKS - 1:
                     busy = psum.tile([P, BANK], F32, name="busy%d%d" % (m, c), tag="bank%d" % (BANKS * m + c))
                     nc.tensor.matmul(out=busy[:], lhsT=left[(0, 0)][:, 0:P], rhs=left[(0, 0)][:, 0:BANK],
                                      start=True, stop=True)
@@ -192,7 +215,10 @@ def tile_builtcontrolled_kernel(tc, state, target_matrix, control, num_qubits, o
 
         n_units = len(units)
         first_of_last_pass = n_units - BANKS
+        waiting = []
         for k in range(n_units + AMAX_LAG):
+            if k + 1 in CHUNK_UNITS:
+                tensor_interleave(k + 1)
             if k < n_units:
                 interleave(k)
             if k == 0:
@@ -202,7 +228,11 @@ def tile_builtcontrolled_kernel(tc, state, target_matrix, control, num_qubits, o
                 x_quant(1, 1)
             if 0 <= k - 1 < n_units:
                 quantize(k - 1)
-                multiply(k - 1)
+                waiting.append(k - 1)
+                for j in list(waiting):
+                    if units[j][1] < BANKS - 1 or k > CHUNK_UNITS[-1]:
+                        multiply(j)
+                        waiting.remove(j)
             if 0 <= k - EVAC_LAG - first_of_last_pass < BANKS:
                 right_evac(k - EVAC_LAG - first_of_last_pass)
             if 0 <= k - AMAX_LAG - first_of_last_pass < BANKS:

@@ -217,8 +217,8 @@ def tile_builtcontrolled_kernel(tc, state, target_matrix, control, num_qubits, o
         first_of_last_pass = n_units - BANKS
         waiting = []
         for k in range(n_units + AMAX_LAG):
-            if k + 1 in CHUNK_UNITS:
-                tensor_interleave(k + 1)
+            if k + 2 in CHUNK_UNITS:
+                tensor_interleave(k + 2)
             if k < n_units:
                 interleave(k)
             if k == 0:

@@ -29,7 +29,7 @@ PIECES = HALF // PIECE
 FLOPS = 2 * ROWS * HALF * HALF
 BYTES = ROWS * DIM * 2 + HALF * HALF * 2 + ROWS * DIM * 4 + ROWS * DIM
 
-LOAD_WIDTHS = ((512, 512, 1024), (1024, 1024), (1024, 1024), (512, 512, 512, 512))
+LOAD_WIDTHS = ((1024, 1024), (1024, 1024), (1024, 1024), (512, 512, 512, 512))
 V_COLS = 240
 CHUNK_UNITS = (3, 5, 7, 9, 11)
 CHUNK_COLS = 256

@@ -6,6 +6,7 @@ from concourse.masks import make_identity
 F32 = mybir.dt.float32
 BF16 = mybir.dt.bfloat16
 U32 = mybir.dt.uint32
+I32 = mybir.dt.int32
 U8 = mybir.dt.uint8
 FP8X4 = mybir.dt.float8_e4m3fn_x4
 FP8 = mybir.dt.float8_e4m3fn
@@ -97,9 +98,18 @@ def tile_builtcontrolled_kernel(tc, state, target_matrix, control, num_qubits, o
         def abs_max(i, src):
             nc.vector.tensor_reduce(out=stats[:, i:i + 1], in_=src, axis=AX.X, op=ALU.max, apply_absolute_value=True)
 
+        def abs_max_bf16(i, src):
+            width = src.shape[1]
+            mag = stage.tile([P, width // 2], I32, name="mag")
+            nc.vector.tensor_scalar(out=mag[:], in0=src.bitcast(I32), scalar1=0x7FFF7FFF, scalar2=None,
+                                    op0=ALU.bitwise_and)
+            same = stage.tile([P, width], BF16, name="same")
+            nc.vector.tensor_scalar(out=same[:], in0=mag[:].bitcast(BF16), scalar1=1.0, scalar2=None, op0=ALU.mult,
+                                    op1=ALU.max, accum_out=stats[:, i:i + 1])
+
         def left_half(m, h):
             cols = slice(PIECE * h, PIECE * (h + 1))
-            abs_max(PIECES * m + h, left[(m, h)])
+            abs_max_bf16(PIECES * m + h, left[(m, h)])
             if m == 0:
                 nc.scalar.copy(out=o[m][:, cols], in_=left[(m, h)])
             else:
@@ -210,8 +220,10 @@ def tile_builtcontrolled_kernel(tc, state, target_matrix, control, num_qubits, o
         x_transpose(1, 0)
         x_transpose(1, 1)
         x_evac(1, 0)
-        x_quant(0, 0)
-        x_quant(0, 1)
+        x_evac(1, 1)
+        for m in range(ROW_TILES):
+            for h in range(PIECES):
+                x_quant(m, h)
 
         n_units = len(units)
         first_of_last_pass = n_units - BANKS
@@ -221,11 +233,6 @@ def tile_builtcontrolled_kernel(tc, state, target_matrix, control, num_qubits, o
                 tensor_interleave(k + 2)
             if k < n_units:
                 interleave(k)
-            if k == 0:
-                x_quant(1, 0)
-                x_evac(1, 1)
-            if k == 1:
-                x_quant(1, 1)
             if 0 <= k - 1 < n_units:
                 quantize(k - 1)
                 waiting.append(k - 1)

@@ -31,7 +31,7 @@ FLOPS = 2 * ROWS * HALF * HALF
 BYTES = ROWS * DIM * 2 + HALF * HALF * 2 + ROWS * DIM * 4 + ROWS * DIM
 
 LOAD_WIDTHS = ((1024, 1024), (1024, 1024), (1024, 1024), (512, 512, 512, 512))
-V_COLS = 240
+V_COLS = 248
 CHUNK_UNITS = (3, 5, 7, 9, 11)
 CHUNK_COLS = 256
 CHUNK_V_COLS = 176
@@ -90,32 +90,38 @@ def tile_builtcontrolled_kernel(tc, state, target_matrix, control, num_qubits, o
         t_scales = keep.tile([P, PASSES * HALF], U8, name="t_scales", align_bytes=64)
         x_codes = keep.tile([P, ROW_TILES * PASSES * P], U32, name="x_codes", align_bytes=64)
         x_scales = keep.tile([P, ROW_TILES * PASSES * P], U8, name="x_scales", align_bytes=64)
-        o = [keep.tile([P, DIM], F32, name="o%d" % m) for m in range(ROW_TILES)]
+        n_stats = ROW_TILES * (PIECES + BANKS) - 1
+        o = [keep.tile([P, DIM + (n_stats if m == ROW_TILES - 1 else 0)], F32, name="o%d" % m) for m in range(ROW_TILES)]
+        stats = o[ROW_TILES - 1][:, DIM:DIM + n_stats]
+        part = keep.tile([P, 1], F32, name="part")
         o8 = [keep.tile([P, DIM], FP8, name="q8%d" % m) for m in range(ROW_TILES)]
-        n_stats = ROW_TILES * (PIECES + BANKS)
-        stats = keep.tile([P, n_stats], F32, name="stats")
 
-        def abs_max(i, src):
-            nc.vector.tensor_reduce(out=stats[:, i:i + 1], in_=src, axis=AX.X, op=ALU.max, apply_absolute_value=True)
+        def abs_max(dst, src):
+            nc.vector.tensor_reduce(out=dst, in_=src, axis=AX.X, op=ALU.max, apply_absolute_value=True)
 
-        def abs_max_bf16(i, src):
-            width = src.shape[1]
-            mag = stage.tile([P, width // 2], I32, name="mag")
+        def clear_signs(src):
+            mag = stage.tile([P, src.shape[1] // 2], I32, name="mag")
             nc.vector.tensor_scalar(out=mag[:], in0=src.bitcast(I32), scalar1=0x7FFF7FFF, scalar2=None,
                                     op0=ALU.bitwise_and)
-            same = stage.tile([P, width], BF16, name="same")
+            return mag
+
+        def max_of(i, mag):
+            same = stage.tile([P, 2 * mag.shape[1]], BF16, name="same")
             nc.vector.tensor_scalar(out=same[:], in0=mag[:].bitcast(BF16), scalar1=1.0, scalar2=None, op0=ALU.mult,
                                     op1=ALU.max, accum_out=stats[:, i:i + 1])
 
-        def left_half(m, h):
-            cols = slice(PIECE * h, PIECE * (h + 1))
-            abs_max_bf16(PIECES * m + h, left[(m, h)])
-            if m == 0:
-                nc.scalar.copy(out=o[m][:, cols], in_=left[(m, h)])
-            else:
-                nc.gpsimd.tensor_scalar(out=o[m][:, cols], in0=left[(m, h)], scalar1=1.0, scalar2=0.0,
-                                        op0=ALU.mult, op1=ALU.add)
-            nc.sync.dma_start(out=out_0[m * P:(m + 1) * P, cols], in_=o[m][:, cols])
+        def left_half(m):
+            mags = [clear_signs(left[(m, h)]) for h in range(PIECES)]
+            for h in range(PIECES):
+                max_of(PIECES * m + h, mags[h])
+            for h in range(PIECES):
+                cols = slice(PIECE * h, PIECE * (h + 1))
+                if m == 0:
+                    nc.scalar.copy(out=o[m][:, cols], in_=left[(m, h)])
+                else:
+                    nc.gpsimd.tensor_scalar(out=o[m][:, cols], in0=left[(m, h)], scalar1=1.0, scalar2=0.0,
+                                            op0=ALU.mult, op1=ALU.add)
+                nc.sync.dma_start(out=out_0[m * P:(m + 1) * P, cols], in_=o[m][:, cols])
 
         xt = {}
         x_grouped = {}
@@ -206,17 +212,19 @@ def tile_builtcontrolled_kernel(tc, state, target_matrix, control, num_qubits, o
         def right_amax_store(c):
             cols = slice(HALF + c * BANK, HALF + (c + 1) * BANK)
             for m in range(ROW_TILES):
-                abs_max(ROW_TILES * PIECES + BANKS * m + c, o[m][:, cols])
+                i = ROW_TILES * (PIECES + c) + m
+                if i < n_stats:
+                    abs_max(stats[:, i:i + 1], o[m][:, cols])
+                else:
+                    abs_max(part[:, 0:1], o[m][:, HALF + c * BANK:DIM + n_stats])
                 nc.sync.dma_start(out=out_0[m * P:(m + 1) * P, cols], in_=o[m][:, cols])
 
-        for h in range(PIECES):
-            left_half(0, h)
+        left_half(0)
         x_transpose(0, 0)
         x_transpose(0, 1)
         x_evac(0, 0)
         x_evac(0, 1)
-        for h in range(PIECES):
-            left_half(1, h)
+        left_half(1)
         x_transpose(1, 0)
         x_transpose(1, 1)
         x_evac(1, 0)
@@ -245,14 +253,12 @@ def tile_builtcontrolled_kernel(tc, state, target_matrix, control, num_qubits, o
             if 0 <= k - AMAX_LAG - first_of_last_pass < BANKS:
                 right_amax_store(k - AMAX_LAG - first_of_last_pass)
 
-        scaled = keep.tile([P, n_stats], F32, name="scaled")
-        part = keep.tile([P, 1], F32, name="part")
-        nc.vector.tensor_scalar(out=scaled[:], in0=stats[:], scalar1=1.0 / 448.0, scalar2=None, op0=ALU.mult,
-                                op1=ALU.max, accum_out=part[:, 0:1])
         spread = psum.tile([P, P], F32, name="spread", tag="bank0")
         nc.tensor.transpose(spread[:], part[:, 0:1].to_broadcast([P, P]), ident[:])
+        scaled = keep.tile([P, P], F32, name="scaled")
         scale = keep.tile([P, 1], F32, name="scale")
-        nc.vector.tensor_reduce(out=scale[:], in_=spread[:], axis=AX.X, op=ALU.max)
+        nc.vector.tensor_scalar(out=scaled[:], in0=spread[:], scalar1=1.0 / 448.0, scalar2=None, op0=ALU.mult,
+                                op1=ALU.max, accum_out=scale[:, 0:1])
         factor = keep.tile([P, 1], F32, name="factor")
         nc.vector.reciprocal(out=factor[:], in_=scale[:])
 

@@ -36,6 +36,7 @@ CHUNK_UNITS = (3, 5, 7, 9, 11)
 CHUNK_COLS = 256
 CHUNK_V_COLS = 176
 CHUNK_BANKS = (3, 7)
+WARM_PASSES = 4
 GROUPED_BUFS = 4
 EVAC_LAG = 2
 AMAX_LAG = 3
@@ -63,15 +64,12 @@ def tile_builtcontrolled_kernel(tc, state, target_matrix, control, num_qubits, o
 
         left = {}
         right = {}
-        for m in range(ROW_TILES):
-            rows = slice(m * P, (m + 1) * P)
-            xl = keep.tile([P, HALF], BF16, name="xl%d" % m)
-            nc.sync.dma_start(out=xl[:], in_=state[rows, 0:HALF])
-            xr = keep.tile([P, HALF], BF16, name="xr%d" % m)
-            nc.sync.dma_start(out=xr[:], in_=state[rows, HALF:DIM])
+        for half, m in ((left, 0), (right, 0), (right, 1), (left, 1)):
+            first = 0 if half is left else HALF
+            x = keep.tile([P, HALF], BF16, name="x%s%d" % ("l" if half is left else "r", m))
+            nc.sync.dma_start(out=x[:], in_=state[m * P:(m + 1) * P, first:first + HALF])
             for h in range(PIECES):
-                left[(m, h)] = xl[:, PIECE * h:PIECE * (h + 1)]
-                right[(m, h)] = xr[:, PIECE * h:PIECE * (h + 1)]
+                half[(m, h)] = x[:, PIECE * h:PIECE * (h + 1)]
         raw_of = {}
         for g in range(PASSES):
             c0 = 0
@@ -90,14 +88,13 @@ def tile_builtcontrolled_kernel(tc, state, target_matrix, control, num_qubits, o
         t_scales = keep.tile([P, PASSES * HALF], U8, name="t_scales", align_bytes=64)
         x_codes = keep.tile([P, ROW_TILES * PASSES * P], U32, name="x_codes", align_bytes=64)
         x_scales = keep.tile([P, ROW_TILES * PASSES * P], U8, name="x_scales", align_bytes=64)
-        n_stats = ROW_TILES * (PIECES + BANKS) - 1
-        o = [keep.tile([P, DIM + (n_stats if m == ROW_TILES - 1 else 0)], F32, name="o%d" % m) for m in range(ROW_TILES)]
-        stats = o[ROW_TILES - 1][:, DIM:DIM + n_stats]
-        part = keep.tile([P, 1], F32, name="part")
+        o = [keep.tile([P, DIM], F32, name="o%d" % m) for m in range(ROW_TILES)]
         o8 = [keep.tile([P, DIM], FP8, name="q8%d" % m) for m in range(ROW_TILES)]
+        n_stats = ROW_TILES * (PIECES + BANKS)
+        stats = keep.tile([P, n_stats], F32, name="stats")
 
-        def abs_max(dst, src):
-            nc.vector.tensor_reduce(out=dst, in_=src, axis=AX.X, op=ALU.max, apply_absolute_value=True)
+        def abs_max(i, src):
+            nc.vector.tensor_reduce(out=stats[:, i:i + 1], in_=src, axis=AX.X, op=ALU.max, apply_absolute_value=True)
 
         def clear_signs(src):
             mag = stage.tile([P, src.shape[1] // 2], I32, name="mag")
@@ -212,11 +209,7 @@ def tile_builtcontrolled_kernel(tc, state, target_matrix, control, num_qubits, o
         def right_amax_store(c):
             cols = slice(HALF + c * BANK, HALF + (c + 1) * BANK)
             for m in range(ROW_TILES):
-                i = ROW_TILES * (PIECES + c) + m
-                if i < n_stats:
-                    abs_max(stats[:, i:i + 1], o[m][:, cols])
-                else:
-                    abs_max(part[:, 0:1], o[m][:, HALF + c * BANK:DIM + n_stats])
+                abs_max(ROW_TILES * PIECES + BANKS * m + c, o[m][:, cols])
                 nc.sync.dma_start(out=out_0[m * P:(m + 1) * P, cols], in_=o[m][:, cols])
 
         left_half(0)
@@ -232,6 +225,18 @@ def tile_builtcontrolled_kernel(tc, state, target_matrix, control, num_qubits, o
         for m in range(ROW_TILES):
             for h in range(PIECES):
                 x_quant(m, h)
+
+        for i in range(WARM_PASSES):
+            warm_bank = psum.tile([P, BANK], F32, name="warm%d" % i, tag="bank0")
+            nc.tensor.matmul_mx(
+                out=warm_bank[:],
+                lhsT=x_codes[:, 0:P].bitcast(FP8X4),
+                lhsT_scale=x_scales[:, 0:P],
+                rhs=x_codes[:, 0:BANK].bitcast(FP8X4),
+                rhs_scale=x_scales[:, 0:BANK],
+                start=True,
+                stop=True,
+            )
 
         n_units = len(units)
         first_of_last_pass = n_units - BANKS
@@ -253,12 +258,14 @@ def tile_builtcontrolled_kernel(tc, state, target_matrix, control, num_qubits, o
             if 0 <= k - AMAX_LAG - first_of_last_pass < BANKS:
                 right_amax_store(k - AMAX_LAG - first_of_last_pass)
 
+        scaled = keep.tile([P, n_stats], F32, name="scaled")
+        part = keep.tile([P, 1], F32, name="part")
+        nc.vector.tensor_scalar(out=scaled[:], in0=stats[:], scalar1=1.0 / 448.0, scalar2=None, op0=ALU.mult,
+                                op1=ALU.max, accum_out=part[:, 0:1])
         spread = psum.tile([P, P], F32, name="spread", tag="bank0")
         nc.tensor.transpose(spread[:], part[:, 0:1].to_broadcast([P, P]), ident[:])
-        scaled = keep.tile([P, P], F32, name="scaled")
         scale = keep.tile([P, 1], F32, name="scale")
-        nc.vector.tensor_scalar(out=scaled[:], in0=spread[:], scalar1=1.0 / 448.0, scalar2=None, op0=ALU.mult,
-                                op1=ALU.max, accum_out=scale[:, 0:1])
+        nc.vector.tensor_reduce(out=scale[:], in_=spread[:], axis=AX.X, op=ALU.max)
         factor = keep.tile([P, 1], F32, name="factor")
         nc.vector.reciprocal(out=factor[:], in_=scale[:])
 

from contextlib import ExitStack

import concourse.mybir as mybir
from concourse.masks import make_identity

F32 = mybir.dt.float32
BF16 = mybir.dt.bfloat16
U32 = mybir.dt.uint32
I32 = mybir.dt.int32
U8 = mybir.dt.uint8
FP8X4 = mybir.dt.float8_e4m3fn_x4
FP8 = mybir.dt.float8_e4m3fn
ALU = mybir.AluOpType
ACT = mybir.ActivationFunctionType
AX = mybir.AxisListType

P = 128
ROWS = 256
DIM = 4096
HALF = 2048
PACK = 4
K_PASS = P * PACK
PASSES = HALF // K_PASS
ROW_TILES = ROWS // P
BANK = 512
BANKS = HALF // BANK
PIECE = 1024
PIECES = HALF // PIECE

FLOPS = 2 * ROWS * HALF * HALF
BYTES = ROWS * DIM * 2 + HALF * HALF * 2 + ROWS * DIM * 4 + ROWS * DIM

LOAD_WIDTHS = ((1024, 1024), (1024, 1024), (1024, 1024), (512, 512, 512, 512))
V_COLS = 248
CHUNK_UNITS = (3, 5, 7, 9, 11)
CHUNK_COLS = 256
CHUNK_V_COLS = 176
CHUNK_BANKS = (3, 7)
WARM_PASSES = 4
GROUPED_BUFS = 4
EVAC_LAG = 2
AMAX_LAG = 3
XT_BANK = {(0, 0): 2, (0, 1): 3, (1, 0): 6, (1, 1): 7}
CAST_PIECES = ((0, 0, 2048), (0, 2048, 2048), (1, 0, 2048), (1, 2048, 1024), (1, 3072, 1024))
CAST_V_SHARE = 0.67


def tile_builtcontrolled_kernel(tc, state, target_matrix, control, num_qubits, out_0, out_1):
    nc = tc.nc
    with ExitStack() as ctx:
        keep = ctx.enter_context(tc.tile_pool(name="keep", bufs=1))
        stage = ctx.enter_context(tc.tile_pool(name="stage", bufs=GROUPED_BUFS))
        psum = ctx.enter_context(tc.psum_pool(name="psum", bufs=1))
        ctx.enter_context(tc.manual_schedule())

        ident = keep.tile([P, P], F32, name="ident")
        make_identity(nc, ident[:])
        ident_bf = keep.tile([P, P], BF16, name="ident_bf")
        make_identity(nc, ident_bf[:])
        zero = keep.tile([P, 1], F32, name="zero")
        nc.vector.memset(zero[:], 0.0)
        warm = keep.tile([P, 1], F32, name="warm")
        nc.scalar.activation(out=warm[:], in_=zero[:], func=ACT.Identity, scale=zero[:, 0:1], bias=zero[:, 0:1])

        left = {}
        right = {}
        for half, m in ((left, 0), (right, 0), (right, 1), (left, 1)):
            first = 0 if half is left else HALF
            x = keep.tile([P, HALF], BF16, name="x%s%d" % ("l" if half is left else "r", m))
            nc.sync.dma_start(out=x[:], in_=state[m * P:(m + 1) * P, first:first + HALF])
            for h in range(PIECES):
                half[(m, h)] = x[:, PIECE * h:PIECE * (h + 1)]
        raw_of = {}
        for g in range(PASSES):
            c0 = 0
            for d, width in enumerate(LOAD_WIDTHS[g]):
                raw = keep.tile([P, PACK, width], BF16, name="raw%d%d" % (g, d))
                nc.sync.dma_start(
                    out=raw[:],
                    in_=target_matrix[HALF + K_PASS * g:HALF + K_PASS * (g + 1), HALF + c0:HALF + c0 + width]
                    .rearrange("(p t) w -> p t w", t=PACK),
                )
                for c in range(c0 // BANK, (c0 + width) // BANK):
                    raw_of[(g, c)] = (raw, c * BANK - c0)
                c0 += width

        t_codes = keep.tile([P, PASSES * HALF], U32, name="t_codes", align_bytes=64)
        t_scales = keep.tile([P, PASSES * HALF], U8, name="t_scales", align_bytes=64)
        x_codes = keep.tile([P, ROW_TILES * PASSES * P], U32, name="x_codes", align_bytes=64)
        x_scales = keep.tile([P, ROW_TILES * PASSES * P], U8, name="x_scales", align_bytes=64)
        o = [keep.tile([P, DIM], F32, name="o%d" % m) for m in range(ROW_TILES)]
        o8 = [keep.tile([P, DIM], FP8, name="q8%d" % m) for m in range(ROW_TILES)]
        n_stats = ROW_TILES * (PIECES + BANKS)
        stats = keep.tile([P, n_stats], F32, name="stats")

        def abs_max(i, src):
            nc.vector.tensor_reduce(out=stats[:, i:i + 1], in_=src, axis=AX.X, op=ALU.max, apply_absolute_value=True)

        def clear_signs(src):
            mag = stage.tile([P, src.shape[1] // 2], I32, name="mag")
            nc.vector.tensor_scalar(out=mag[:], in0=src.bitcast(I32), scalar1=0x7FFF7FFF, scalar2=None,
                                    op0=ALU.bitwise_and)
            return mag

        def max_of(i, mag):
            same = stage.tile([P, 2 * mag.shape[1]], BF16, name="same")
            nc.vector.tensor_scalar(out=same[:], in0=mag[:].bitcast(BF16), scalar1=1.0, scalar2=None, op0=ALU.mult,
                                    op1=ALU.max, accum_out=stats[:, i:i + 1])

        def left_half(m):
            mags = [clear_signs(left[(m, h)]) for h in range(PIECES)]
            for h in range(PIECES):
                max_of(PIECES * m + h, mags[h])
            for h in range(PIECES):
                cols = slice(PIECE * h, PIECE * (h + 1))
                if m == 0:
                    nc.scalar.copy(out=o[m][:, cols], in_=left[(m, h)])
                else:
                    nc.gpsimd.tensor_scalar(out=o[m][:, cols], in0=left[(m, h)], scalar1=1.0, scalar2=0.0,
                                            op0=ALU.mult, op1=ALU.add)
                nc.sync.dma_start(out=out_0[m * P:(m + 1) * P, cols], in_=o[m][:, cols])

        xt = {}
        x_grouped = {}

        def x_transpose(m, h):
            words = right[(m, h)].bitcast(F32)
            xt[(m, h)] = psum.tile([P, 2, 2, P], F32, name="xt%d%d" % (m, h), tag="bank%d" % XT_BANK[(m, h)])
            for gi in range(2):
                for u in range(2):
                    nc.tensor.transpose(xt[(m, h)][:, gi, u, :], words[:, 256 * gi + u:256 * (gi + 1):2], ident[:])

        def x_evac(m, h):
            x_grouped[(m, h)] = keep.tile([P, 2, P, PACK], BF16, name="xg%d%d" % (m, h), align_bytes=64)
            nc.scalar.copy(out=x_grouped[(m, h)][:].bitcast(F32), in_=xt[(m, h)][:].rearrange("p g u r -> p g r u"))

        def x_quant(m, h):
            base = (m * PASSES + 2 * h) * P
            nc.vector.quantize_mx(
                out=x_codes[:, base:base + 2 * P].bitcast(FP8X4),
                scales=x_scales[:, base:base + 2 * P],
                in_=x_grouped[(m, h)][:].rearrange("p g r t -> p (g r t)"),
            )

        units = [(g, c) for g in range(PASSES) for c in range(BANKS)]
        grouped = {}
        acc = {}

        def interleave(k):
            raw, c0 = raw_of[units[k]]
            grp = stage.tile([P, BANK, PACK], BF16, name="grp", align_bytes=64)
            grouped[k] = grp
            v_end = CHUNK_V_COLS if k in CHUNK_UNITS else V_COLS
            s_end = BANK - CHUNK_COLS if k in CHUNK_UNITS else BANK
            nc.vector.tensor_copy(out=grp[:, 0:v_end, :].rearrange("p (c i) t -> p c t i", i=4),
                                  in_=raw[:, :, c0:c0 + v_end].rearrange("p t (c i) -> p c t i", i=4))
            nc.scalar.copy(out=grp[:, v_end:s_end, :].rearrange("p (c i) t -> p c t i", i=4),
                           in_=raw[:, :, c0 + v_end:c0 + s_end].rearrange("p t (c i) -> p c t i", i=4))
            if k in CHUNK_UNITS:
                nc.scalar.copy(out=grp[:, s_end:BANK, :].rearrange("p w t -> p (w t)"), in_=chunk[k][:])

        chunk = {}

        def tensor_interleave(k):
            raw, c0 = raw_of[units[k]]
            first = c0 + BANK - CHUNK_COLS
            chunk[k] = psum.tile([P, CHUNK_COLS * PACK], BF16, name="chunk%d" % k,
                                 tag="bank%d" % CHUNK_BANKS[CHUNK_UNITS.index(k) % len(CHUNK_BANKS)])
            for j in range(CHUNK_COLS // P):
                nc.tensor.matmul(out=chunk[k][:, BANK * j:BANK * (j + 1)].rearrange("p (w t) -> p w t", t=PACK),
                                 lhsT=ident_bf[:],
                                 rhs=raw[:, :, first + P * j:first + P * (j + 1)].rearrange("p t w -> p w t"),
                                 start=True, stop=True)

        def quantize(k):
            g, c = units[k]
            tb = g * HALF + c * BANK
            nc.vector.quantize_mx(
                out=t_codes[:, tb:tb + BANK].bitcast(FP8X4),
                scales=t_scales[:, tb:tb + BANK],
                in_=grouped[k][:].rearrange("p w t -> p (w t)"),
            )

        def multiply(k):
            g, c = units[k]
            tb = g * HALF + c * BANK
            for m in range(ROW_TILES):
                if g == 0:
                    acc[(m, c)] = psum.tile([P, BANK], F32, name="acc%d%d" % (m, c), tag="bank%d" % (BANKS * m + c))
                xb = (m * PASSES + g) * P
                nc.tensor.matmul_mx(
                    out=acc[(m, c)][:],
                    lhsT=x_codes[:, xb:xb + P].bitcast(FP8X4),
                    lhsT_scale=x_scales[:, xb:xb + P],
                    rhs=t_codes[:, tb:tb + BANK].bitcast(FP8X4),
                    rhs_scale=t_scales[:, tb:tb + BANK],
                    start=(g == 0),
                    stop=(g == PASSES - 1),
                )

        def right_evac(c):
            for m in range(ROW_TILES):
                nc.scalar.copy(out=o[m][:, HALF + c * BANK:HALF + (c + 1) * BANK], in_=acc[(m, c)][:])
                if c >= BANKS - 1:
                    busy = psum.tile([P, BANK], F32, name="busy%d%d" % (m, c), tag="bank%d" % (BANKS * m + c))
                    nc.tensor.matmul(out=busy[:], lhsT=left[(0, 0)][:, 0:P], rhs=left[(0, 0)][:, 0:BANK],
                                     start=True, stop=True)

        def right_amax_store(c):
            cols = slice(HALF + c * BANK, HALF + (c + 1) * BANK)
            for m in range(ROW_TILES):
                abs_max(ROW_TILES * PIECES + BANKS * m + c, o[m][:, cols])
                nc.sync.dma_start(out=out_0[m * P:(m + 1) * P, cols], in_=o[m][:, cols])

        left_half(0)
        x_transpose(0, 0)
        x_transpose(0, 1)
        x_evac(0, 0)
        x_evac(0, 1)
        left_half(1)
        x_transpose(1, 0)
        x_transpose(1, 1)
        x_evac(1, 0)
        x_evac(1, 1)
        for m in range(ROW_TILES):
            for h in range(PIECES):
                x_quant(m, h)

        for i in range(WARM_PASSES):
            warm_bank = psum.tile([P, BANK], F32, name="warm%d" % i, tag="bank0")
            nc.tensor.matmul_mx(
                out=warm_bank[:],
                lhsT=x_codes[:, 0:P].bitcast(FP8X4),
                lhsT_scale=x_scales[:, 0:P],
                rhs=x_codes[:, 0:BANK].bitcast(FP8X4),
                rhs_scale=x_scales[:, 0:BANK],
                start=True,
                stop=True,
            )

        n_units = len(units)
        first_of_last_pass = n_units - BANKS
        waiting = []
        for k in range(n_units + AMAX_LAG):
            if k + 2 in CHUNK_UNITS:
                tensor_interleave(k + 2)
            if k < n_units:
                interleave(k)
            if 0 <= k - 1 < n_units:
                quantize(k - 1)
                waiting.append(k - 1)
                for j in list(waiting):
                    if units[j][1] < BANKS - 1 or k > CHUNK_UNITS[-1]:
                        multiply(j)
                        waiting.remove(j)
            if 0 <= k - EVAC_LAG - first_of_last_pass < BANKS:
                right_evac(k - EVAC_LAG - first_of_last_pass)
            if 0 <= k - AMAX_LAG - first_of_last_pass < BANKS:
                right_amax_store(k - AMAX_LAG - first_of_last_pass)

        scaled = keep.tile([P, n_stats], F32, name="scaled")
        part = keep.tile([P, 1], F32, name="part")
        nc.vector.tensor_scalar(out=scaled[:], in0=stats[:], scalar1=1.0 / 448.0, scalar2=None, op0=ALU.mult,
                                op1=ALU.max, accum_out=part[:, 0:1])
        spread = psum.tile([P, P], F32, name="spread", tag="bank0")
        nc.tensor.transpose(spread[:], part[:, 0:1].to_broadcast([P, P]), ident[:])
        scale = keep.tile([P, 1], F32, name="scale")
        nc.vector.tensor_reduce(out=scale[:], in_=spread[:], axis=AX.X, op=ALU.max)
        factor = keep.tile([P, 1], F32, name="factor")
        nc.vector.reciprocal(out=factor[:], in_=scale[:])

        for m, a, width in CAST_PIECES:
            vw = int(width * CAST_V_SHARE) // 16 * 16
            nc.vector.tensor_scalar(out=o8[m][:, a:a + vw], in0=o[m][:, a:a + vw], scalar1=factor[:, 0:1],
                                    scalar2=None, op0=ALU.mult, saturate=False)
            nc.scalar.activation(out=o8[m][:, a + vw:a + width], in_=o[m][:, a + vw:a + width], func=ACT.Identity,
                                 scale=factor[:, 0:1], bias=zero[:, 0:1], saturate=False)
            nc.sync.dma_start(out=out_1[m * P:(m + 1) * P, a:a + width], in_=o8[m][:, a:a + width].bitcast(U8))
